import numpy as np
import ml_dtypes


def mxq(x, axis, fmt="e4m3"):
    dtype, down = {"e4m3": (ml_dtypes.float8_e4m3fn, 7), "e5m2": (ml_dtypes.float8_e5m2, 14)}[fmt]
    v = np.moveaxis(np.asarray(x, np.float32).astype(ml_dtypes.bfloat16).astype(np.float64), axis, -1)
    blocks = v.reshape(v.shape[:-1] + (-1, 32))
    amax = np.abs(blocks).max(-1, keepdims=True)
    byte = np.maximum(np.where(amax > 0, np.frexp(amax)[1] - 1 + 127, 0) - down, 1)
    scale = np.exp2(byte - 127.0)
    codes = (blocks / scale).astype(np.float32).astype(dtype).astype(np.float64)
    return np.moveaxis((codes * scale).reshape(v.shape), -1, axis)


WIDE = False


def mx_kscale(k):
    if not WIDE:
        return np.ones(k)
    levels = np.array([10, -10, 5, -5, 0])
    a = np.random.permutation(np.resize(levels, k // 512 * 4)).reshape(k // 512, 4)
    idx = np.arange(k)
    return np.exp2(a[idx // 512, idx % 128 // 32])


BF16 = ml_dtypes.bfloat16


def bf(x):
    return np.asarray(x, np.float32).astype(BF16)


def f64(x):
    return np.asarray(x).astype(np.float64)


B, T, N, H = 4, 2048, 512, 1024
MIN_NORM = 1e-15
PROJ_EPS = 0.004
C = 1.0
SQRT_C = 1.0


def artanh(x):
    x = np.clip(x, -1.0 + 1e-7, 1.0 - 1e-7)
    return 0.5 * (np.log(1.0 + x) - np.log(1.0 - x))


def _norm(x):
    return np.maximum(np.sqrt((x * x).sum(-1, keepdims=True)), MIN_NORM)


def proj(x):
    norm = _norm(x)
    maxnorm = (1.0 - PROJ_EPS) / SQRT_C
    return np.where(norm > maxnorm, x / norm * maxnorm, x)


def expmap0(u):
    u_norm = _norm(u)
    return np.tanh(SQRT_C * u_norm) * u / (SQRT_C * u_norm)


def logmap0(p):
    p_norm = _norm(p)
    return artanh(SQRT_C * p_norm) * p / (SQRT_C * p_norm)


def mobius_add(x, y):
    x2 = (x * x).sum(-1, keepdims=True)
    y2 = (y * y).sum(-1, keepdims=True)
    xy = (x * y).sum(-1, keepdims=True)
    num = (1.0 + 2.0 * C * xy + C * y2) * x + (1.0 - C * x2) * y
    denom = 1.0 + 2.0 * C * xy + C * C * x2 * y2
    return num / np.maximum(denom, MIN_NORM)


def setup_inputs():
    s = mx_kscale(H)
    c = np.exp2(np.round(np.log2(np.sqrt(np.mean(s * s)))))
    rho = 0.3 + 0.9 * np.random.random((B, N, 1))
    x1 = np.maximum(np.random.standard_normal((B, N, H)), 0.0) * np.sqrt(2.0 / H) * rho
    g = np.abs(np.random.standard_normal((B, N, N)))
    A = (g + g.transpose(0, 2, 1)) * 0.25 / np.sqrt(N) + 1.8 * np.eye(N)[None]
    dinv = A.sum(-1) ** -0.5
    adj = dinv[:, :, None] * A * dinv[:, None, :]
    return {"adj": bf(adj), "x1": bf(x1 * s / c),
            "W2": bf(np.random.standard_normal((H, H)) / np.sqrt(H) * c / s[:, None]),
            "b2": bf(np.random.standard_normal(H) * 0.6 / np.sqrt(H))}


def reference(adj, x1, W2, b2):
    x = f64(x1)
    x_norm = _norm(x)
    mx = mxq(x, 2, "e4m3") @ mxq(f64(W2), 0, "e4m3")
    mx_norm = _norm(mx)
    res = np.tanh(mx_norm / x_norm * artanh(SQRT_C * x_norm)) * mx / (mx_norm * SQRT_C)
    res = np.where(np.all(mx == 0, axis=-1, keepdims=True), 0.0, res)
    hyp_bias = proj(expmap0(f64(b2)[None, None, :]))
    support = proj(mobius_add(res, hyp_bias))
    tangent = logmap0(support)
    agg = mxq(f64(adj), 2, "e4m3") @ mxq(tangent, 1, "e4m3")
    return np.maximum(agg, 0.0)

@@ -1,0 +1,397 @@
+import math
+from contextlib import ExitStack
+
+import concourse.mybir as mybir
+from concourse.masks import make_identity
+
+F32 = mybir.dt.float32
+BF16 = mybir.dt.bfloat16
+U32 = mybir.dt.uint32
+U8 = mybir.dt.uint8
+FP8X4 = mybir.dt.float8_e4m3fn_x4
+ALU = mybir.AluOpType
+ACT = mybir.ActivationFunctionType
+
+P = 128
+PACK = 4
+BANK = 512
+GRAPHS, NODES, FEATS = 4, 512, 1024
+TILES_PER_GRAPH = NODES // P
+ROW_TILES = GRAPHS * TILES_PER_GRAPH
+K_PASSES = FEATS // (P * PACK)
+HALVES = FEATS // BANK
+GROUPS = 2
+GROUP_TILES = ROW_TILES // GROUPS
+GRAPHS_PER_GROUP = GRAPHS // GROUPS
+
+MIN_NORM_SQ = 1e-30
+MAX_NORM = 0.996
+ARTANH_CLIP = 1.0 - 1e-7
+
+FLOPS = 2 * GRAPHS * NODES * FEATS * FEATS + 2 * GRAPHS * NODES * NODES * FEATS
+
+
+def tile_module_1_pb_kernel(tc, adj, x1, W2, b2, out):
+    nc = tc.nc
+    with ExitStack() as ctx:
+        const = ctx.enter_context(tc.tile_pool(name="const", bufs=1))
+        keep = ctx.enter_context(tc.tile_pool(name="keep", bufs=1))
+        small = ctx.enter_context(tc.tile_pool(name="small", bufs=1))
+        stage = ctx.enter_context(tc.tile_pool(name="stage", bufs=3))
+        unread = ctx.enter_context(tc.tile_pool(name="unread", bufs=2))
+        tan_pool = ctx.enter_context(tc.tile_pool(name="tan", bufs=2))
+        bias_pool = ctx.enter_context(tc.tile_pool(name="bias", bufs=4))
+        out_pool = ctx.enter_context(tc.tile_pool(name="outs", bufs=4))
+        flip_psum = ctx.enter_context(tc.psum_pool(name="flip", bufs=2))
+        mx_psum = ctx.enter_context(tc.psum_pool(name="mx", bufs=4))
+        agg_psum = ctx.enter_context(tc.psum_pool(name="agg", bufs=2))
+
+        x_nat = keep.tile([P, ROW_TILES, FEATS], BF16)
+        w_raw = keep.tile([P, K_PASSES, PACK, FEATS], BF16)
+        a_nat = keep.tile([P, GRAPHS, TILES_PER_GRAPH, NODES], BF16)
+
+        def load_x(b):
+            cols = slice(b * TILES_PER_GRAPH, (b + 1) * TILES_PER_GRAPH)
+            nc.sync.dma_start(
+                out=x_nat[:, cols, :].rearrange("p (u e) k -> p u (e k)", e=2),
+                in_=x1[b].rearrange("(u p e) k -> p u (e k)", u=2, e=2),
+            )
+
+        def load_w(g):
+            rows = slice(g * P * PACK, (g + 1) * P * PACK)
+            nc.sync.dma_start(
+                out=w_raw[:, g, :, :].rearrange("p (u e) n -> p u (e n)", e=2),
+                in_=W2[rows, :].rearrange("(u p e) n -> p u (e n)", u=2, e=2),
+            )
+
+        b2_row = const.tile([P, FEATS], BF16)
+        nc.vector.memset(b2_row[:], 0.0)
+        nc.sync.dma_start(out=b2_row[0:1, :], in_=b2.rearrange("(o h) -> o h", o=1))
+        load_x(0)
+        load_w(0)
+        load_w(1)
+        load_x(1)
+        load_x(2)
+        load_x(3)
+        for b in range(GRAPHS):
+            nc.sync.dma_start(
+                out=a_nat[:, b, :, :].rearrange("p m j -> p (m j)"),
+                in_=adj[b].rearrange("(p m) j -> p (m j)", m=TILES_PER_GRAPH),
+            )
+
+        ones = const.tile([P, P], BF16)
+        nc.vector.memset(ones[:], 1.0)
+        one_half = const.tile([P, 1], F32)
+        nc.gpsimd.memset(one_half[:], 0.5)
+        ident = const.tile([P, P], F32)
+        make_identity(nc, ident[:])
+        neg_half = const.tile([P, GROUP_TILES], F32)
+        nc.gpsimd.memset(neg_half[:], -0.5)
+        neg_one = const.tile([P, GROUP_TILES], F32)
+        nc.gpsimd.memset(neg_one[:], -1.0)
+        gain_consts = const.tile([P, 2, GROUP_TILES], F32)
+        nc.gpsimd.memset(gain_consts[:, 0, :], 0.5)
+        nc.gpsimd.memset(gain_consts[:, 1, :], 2.0)
+        warm = const.tile([P, 1], F32)
+        nc.scalar.activation(out=warm[:], in_=one_half[:], func=ACT.Ln)
+
+        def g_op(o, a, b, op):
+            nc.gpsimd.tensor_tensor(out=o, in0=a, in1=b, op=op)
+
+        def g_mul(o, a, b):
+            g_op(o, a, b, ALU.mult)
+
+        def g_pow(o, a, exponent):
+            g_op(o, a, exponent, ALU.pow)
+
+        def g_affine(o, a, mul, add):
+            nc.gpsimd.tensor_scalar(out=o, in0=a, scalar1=mul, scalar2=add, op0=ALU.mult, op1=ALU.add)
+
+        def g_one(o, a, scalar, op):
+            nc.gpsimd.tensor_scalar(out=o, in0=a, scalar1=scalar, scalar2=None, op0=op)
+
+        b2_banks = []
+        bn_parts = small.tile([P, HALVES], F32)
+        for h in range(HALVES):
+            b2_bank = mx_psum.tile([P, BANK], F32, name="acc")
+            nc.tensor.matmul(out=b2_bank[:], lhsT=ones[:], rhs=b2_row[:, h * BANK : (h + 1) * BANK], start=True, stop=True)
+            sq_b = unread.tile([P, BANK], BF16, name="sq_s")
+            nc.scalar.activation(out=sq_b[:], in_=b2_bank[:], func=ACT.Square, accum_out=bn_parts[:, h : h + 1])
+            b2_banks.append(b2_bank)
+        bn = small.tile([P, 1], F32)
+        inv_bn = small.tile([P, 1], F32)
+        decay = small.tile([P, 1], F32)
+        hb_norm = small.tile([P, 1], F32)
+        hb_scale = small.tile([P, 1], F32)
+        y2 = small.tile([P, 1], F32)
+        g_op(bn[:], bn_parts[:, 0:1], bn_parts[:, 1:2], ALU.add)
+        g_one(bn[:], bn[:], MIN_NORM_SQ, ALU.max)
+        g_pow(inv_bn[:], bn[:], neg_half[:, 0:1])
+        g_mul(bn[:], bn[:], inv_bn[:])
+        g_one(bn[:], bn[:], 2.0 / math.log(2.0), ALU.mult)
+        g_pow(decay[:], one_half[:], bn[:])
+        g_affine(hb_norm[:], decay[:], 1.0, 1.0)
+        g_pow(hb_norm[:], hb_norm[:], neg_one[:, 0:1])
+        g_affine(decay[:], decay[:], -1.0, 1.0)
+        g_mul(hb_norm[:], hb_norm[:], decay[:])
+        g_one(hb_norm[:], hb_norm[:], MAX_NORM, ALU.min)
+        g_mul(hb_scale[:], hb_norm[:], inv_bn[:])
+        g_mul(y2[:], hb_norm[:], hb_norm[:])
+
+        def regroup(dst, src):
+            nc.vector.tensor_copy(
+                out=dst.rearrange("p (c i) t -> p c t i", i=4),
+                in_=src.rearrange("p t (c i) -> p c t i", i=4),
+            )
+
+        def quantise(grouped, codes, scales):
+            nc.vector.quantize_mx(out=codes.bitcast(FP8X4), scales=scales, in_=grouped)
+
+        def flip(words, copy_out):
+            flipped = flip_psum.tile([P, 4, P], F32)
+            for c in range(4):
+                nc.tensor.transpose(out=flipped[:, c, :], in_=words[:, c * P : (c + 1) * P], identity=ident[:])
+            grouped = stage.tile([P, 2 * P * PACK], BF16, align_bytes=64)
+            copy_out(
+                out=grouped[:].bitcast(F32).rearrange("p (a r u) -> p a r u", a=2, u=2),
+                in_=flipped[:].rearrange("p (a u) r -> p a r u", u=2),
+            )
+            return grouped
+
+        w_codes = keep.tile([P, K_PASSES, FEATS], U32, align_bytes=64)
+        w_scales = keep.tile([P, K_PASSES, FEATS], U8, align_bytes=64)
+        waiting = None
+        for h in range(HALVES):
+            for g in range(K_PASSES):
+                cols = slice(h * BANK, (h + 1) * BANK)
+                w_grouped = stage.tile([P, BANK, PACK], BF16, align_bytes=64)
+                regroup(w_grouped[:], w_raw[:, g, :, cols])
+                if waiting is not None:
+                    quantise(*waiting)
+                waiting = (w_grouped[:].rearrange("p c t -> p (c t)"), w_codes[:, g, cols], w_scales[:, g, cols])
+        quantise(*waiting)
+
+        hb = const.tile([P, FEATS], F32)
+        for h in range(HALVES):
+            nc.vector.tensor_scalar(
+                out=hb[:, h * BANK : (h + 1) * BANK], in0=b2_banks[h][:], scalar1=hb_scale[:, 0:1], scalar2=None, op0=ALU.mult
+            )
+
+        x_codes = keep.tile([P, ROW_TILES, K_PASSES * P], U32, align_bytes=64)
+        x_scales = keep.tile([P, ROW_TILES, K_PASSES * P], U8, align_bytes=64)
+
+        def project(col, h):
+            acc = mx_psum.tile([P, BANK], F32)
+            for g in range(K_PASSES):
+                nc.tensor.matmul_mx(
+                    out=acc[:],
+                    lhsT=x_codes[:, col, g * P : (g + 1) * P].bitcast(FP8X4),
+                    lhsT_scale=x_scales[:, col, g * P : (g + 1) * P],
+                    rhs=w_codes[:, g, h * BANK : (h + 1) * BANK].bitcast(FP8X4),
+                    rhs_scale=w_scales[:, g, h * BANK : (h + 1) * BANK],
+                    start=(g == 0),
+                    stop=(g == K_PASSES - 1),
+                )
+            return acc
+
+        n = GROUP_TILES
+        scalars = [{} for grp in range(GROUPS)]
+
+        def single(grp, label):
+            scalars[grp][label] = small.tile([P, n], F32, name="%s%d" % (label, grp))
+            return scalars[grp][label]
+
+        def double(grp, label):
+            scalars[grp][label] = small.tile([P, 2, n], F32, name="%s%d" % (label, grp))
+            return scalars[grp][label]
+
+        def both(ap):
+            return ap.unsqueeze(1).to_broadcast([P, 2, n])
+
+        def norms_and_codes(grp, copy_out):
+            xn_sq = single(grp, "xn_sq")
+            waiting = None
+            for i in range(n):
+                col = grp * n + i
+                sq_x = unread.tile([P, FEATS], BF16)
+                nc.scalar.activation(out=sq_x[:], in_=x_nat[:, col, :], func=ACT.Square, accum_out=xn_sq[:, i : i + 1])
+                grouped = flip(x_nat[:, col, :].bitcast(F32), copy_out)
+                if waiting is not None:
+                    quantise(*waiting)
+                waiting = (grouped[:], x_codes[:, col, :], x_scales[:, col, :])
+            quantise(*waiting)
+
+        def x_scalars(grp):
+            xn = scalars[grp]["xn_sq"]
+            inv_xn = single(grp, "inv_xn")
+            zb = single(grp, "zb")
+            g_one(xn[:], xn[:], MIN_NORM_SQ, ALU.max)
+            g_pow(inv_xn[:], xn[:], neg_half[:])
+            g_mul(xn[:], xn[:], inv_xn[:])
+            g_one(xn[:], xn[:], ARTANH_CLIP, ALU.min)
+            g_affine(zb[:], xn[:], 1.0, 1.0)
+            g_pow(zb[:], zb[:], neg_one[:])
+            g_affine(xn[:], xn[:], -1.0, 1.0)
+            g_mul(zb[:], zb[:], xn[:])
+
+        def sums(grp):
+            mn_parts = small.tile([P, n, HALVES], F32, name="mn_parts%d" % grp)
+            dot_parts = small.tile([P, n, HALVES], F32, name="dot_parts%d" % grp)
+            scalars[grp]["mn_parts"] = mn_parts
+            scalars[grp]["dot_parts"] = dot_parts
+            for i in range(n):
+                for h in range(HALVES):
+                    acc = project(grp * n + i, h)
+                    prod_v = unread.tile([P, BANK], F32)
+                    nc.vector.scalar_tensor_tensor(
+                        out=prod_v[:], in0=acc[:], scalar=2.0, in1=hb[:, h * BANK : (h + 1) * BANK],
+                        op0=ALU.mult, op1=ALU.mult, accum_out=dot_parts[:, i, h : h + 1],
+                    )
+                    sq_s = unread.tile([P, BANK], BF16)
+                    nc.scalar.activation(out=sq_s[:], in_=acc[:], func=ACT.Square, accum_out=mn_parts[:, i, h : h + 1])
+
+        def start_scalars(grp):
+            got = scalars[grp]
+            mn_e2 = double(grp, "mn_e2")
+            mn, e2 = mn_e2[:, 0, :], mn_e2[:, 1, :]
+            g_op(mn, got["mn_parts"][:, :, 0], got["mn_parts"][:, :, 1], ALU.add)
+            g_op(e2, got["dot_parts"][:, :, 0], got["dot_parts"][:, :, 1], ALU.add)
+            g_one(mn, mn, MIN_NORM_SQ, ALU.max)
+            inv_mn = single(grp, "inv_mn")
+            g_pow(inv_mn[:], mn, neg_half[:])
+            g_mul(mn_e2[:], mn_e2[:], both(inv_mn[:]))
+            z = single(grp, "z")
+            g_mul(z[:], mn, got["inv_xn"][:])
+            g_pow(z[:], got["zb"][:], z[:])
+            p_q = double(grp, "p_q")
+            p, q = p_q[:, 0, :], p_q[:, 1, :]
+            g_affine(p, z[:], -1.0, 1.0)
+            g_affine(q, z[:], 1.0, 1.0)
+            squares = double(grp, "squares")
+            g_mul(squares[:], p_q[:], p_q[:])
+            c1 = single(grp, "c1")
+            g_mul(c1[:], p, q)
+            g_mul(c1[:], c1[:], e2)
+            times_y2 = double(grp, "times_y2")
+            g_one(times_y2[:], squares[:], y2[:, 0:1], ALU.mult)
+            g_op(squares[:], squares[:], both(c1[:]), ALU.add)
+            den = single(grp, "den")
+            g_op(den[:], squares[:, 1, :], times_y2[:, 0, :], ALU.add)
+            nums = double(grp, "nums")
+            g_op(nums[:], squares[:], both(times_y2[:, 1, :]), ALU.add)
+            inv_den_q = single(grp, "inv_den_q")
+            g_mul(den[:], den[:], q)
+            g_pow(inv_den_q[:], den[:], neg_one[:])
+            inv_den = single(grp, "inv_den")
+            g_mul(inv_den[:], inv_den_q[:], q)
+            sn = single(grp, "sn")
+            g_mul(sn[:], nums[:, 0, :], inv_den[:])
+            g_one(sn[:], sn[:], MIN_NORM_SQ, ALU.max)
+            inv_sn = single(grp, "inv_sn")
+            g_pow(inv_sn[:], sn[:], neg_half[:])
+            g_mul(sn[:], sn[:], inv_sn[:])
+            g_one(sn[:], sn[:], MAX_NORM, ALU.min)
+            log_args = double(grp, "log_args")
+            g_affine(log_args[:, 0, :], sn[:], 1.0, 1.0)
+            g_affine(log_args[:, 1, :], sn[:], -1.0, 1.0)
+            factors = double(grp, "factors")
+            g_mul(factors[:, 0, :], nums[:, 1, :], p)
+            g_mul(factors[:, 0, :], factors[:, 0, :], inv_den_q[:])
+            g_mul(factors[:, 0, :], factors[:, 0, :], inv_mn[:])
+            g_mul(factors[:, 1, :], z[:], inv_den[:])
+            g_mul(factors[:], factors[:], both(inv_sn[:]))
+            g_mul(factors[:], factors[:], gain_consts[:])
+
+        def finish_scalars(grp):
+            got = scalars[grp]
+            logs = double(grp, "logs")
+            nc.scalar.activation(out=logs[:], in_=got["log_args"][:], func=ACT.Ln)
+            log_ratio = single(grp, "log_ratio")
+            g_op(log_ratio[:], logs[:, 0, :], logs[:, 1, :], ALU.subtract)
+            alpha_beta = double(grp, "alpha_beta")
+            g_mul(alpha_beta[:], got["factors"][:], both(log_ratio[:]))
+
+        norms_and_codes(0, nc.scalar.copy)
+        x_scalars(0)
+        sums(0)
+        start_scalars(0)
+        norms_and_codes(1, nc.vector.tensor_copy)
+        x_scalars(1)
+        sums(1)
+        finish_scalars(0)
+        start_scalars(1)
+
+        a_codes = keep.tile([P, GRAPHS, NODES], U32, align_bytes=64)
+        a_scales = keep.tile([P, GRAPHS, NODES], U8, align_bytes=64)
+        waiting = None
+        for b in range(GRAPHS):
+            for pair in range(TILES_PER_GRAPH // 2):
+                cols = slice(pair * 2 * P, (pair + 1) * 2 * P)
+                words = a_nat[:, b, 2 * pair : 2 * pair + 2, :].rearrange("p m j -> p (m j)").bitcast(F32)
+                grouped = flip(words, nc.vector.tensor_copy)
+                if waiting is not None:
+                    quantise(*waiting)
+                waiting = (grouped[:], a_codes[:, b, cols], a_scales[:, b, cols])
+        quantise(*waiting)
+
+        tangent = [{} for b in range(GRAPHS)]
+
+        def tangent_tile(b, t):
+            if t == 0:
+                tangent[b]["planes"] = tan_pool.tile([P, PACK, FEATS], BF16, name="planes")
+            grp, i = divmod(b * TILES_PER_GRAPH + t, n)
+            alpha_beta = scalars[grp]["alpha_beta"]
+            beta_hb = bias_pool.tile([P, FEATS], F32)
+            nc.scalar.activation(out=beta_hb[:], in_=hb[:], func=ACT.Copy, scale=alpha_beta[:, 1, i : i + 1])
+            for h in range(HALVES):
+                cols = slice(h * BANK, (h + 1) * BANK)
+                acc = project(b * TILES_PER_GRAPH + t, h)
+                nc.vector.scalar_tensor_tensor(
+                    out=tangent[b]["planes"][:, t, cols], in0=acc[:], scalar=alpha_beta[:, 0, i : i + 1], in1=beta_hb[:, cols],
+                    op0=ALU.mult, op1=ALU.add,
+                )
+
+        def quantise_tangent(b):
+            planes = tangent[b]["planes"]
+            t_grouped = tan_pool.tile([P, FEATS, PACK], BF16, align_bytes=64)
+            t_codes = tan_pool.tile([P, FEATS], U32, align_bytes=64)
+            t_scales = tan_pool.tile([P, FEATS], U8, align_bytes=64)
+            for h in range(HALVES):
+                cols = slice(h * BANK, (h + 1) * BANK)
+                regroup(t_grouped[:, cols, :], planes[:, :, cols])
+            for h in range(HALVES):
+                cols = slice(h * BANK, (h + 1) * BANK)
+                quantise(t_grouped[:, cols, :].rearrange("p c t -> p (c t)"), t_codes[:, cols], t_scales[:, cols])
+            tangent[b]["codes"] = t_codes
+            tangent[b]["scales"] = t_scales
+
+        def aggregate_tile(b, m):
+            result = out_pool.tile([P, FEATS], F32)
+            for h in range(HALVES):
+                cols = slice(h * BANK, (h + 1) * BANK)
+                agg = agg_psum.tile([P, BANK], F32)
+                nc.tensor.matmul_mx(
+                    out=agg[:],
+                    lhsT=a_codes[:, b, m * P : (m + 1) * P].bitcast(FP8X4),
+                    lhsT_scale=a_scales[:, b, m * P : (m + 1) * P],
+                    rhs=tangent[b]["codes"][:, cols].bitcast(FP8X4),
+                    rhs_scale=tangent[b]["scales"][:, cols],
+                    start=True,
+                    stop=True,
+                )
+                nc.scalar.activation(out=result[:, cols], in_=agg[:], func=ACT.Relu)
+            nc.sync.dma_start(out=out[b].rearrange("(p m) f -> p m f", m=TILES_PER_GRAPH)[:, m, :], in_=result[:])
+
+        for t in range(TILES_PER_GRAPH):
+            tangent_tile(0, t)
+        quantise_tangent(0)
+        for b in range(GRAPHS):
+            following = b + 1
+            if following == GRAPHS_PER_GROUP:
+                finish_scalars(1)
+            for t in range(TILES_PER_GRAPH):
+                if following < GRAPHS:
+                    tangent_tile(following, t)
+                aggregate_tile(b, t)
+            if following < GRAPHS:
+                quantise_tangent(following)

@@ -42,9 +42,8 @@ def tile_module_1_pb_kernel(tc, adj, x1, W2, b2, out):
         tan_pool = ctx.enter_context(tc.tile_pool(name="tan", bufs=2))
         bias_pool = ctx.enter_context(tc.tile_pool(name="bias", bufs=4))
         out_pool = ctx.enter_context(tc.tile_pool(name="outs", bufs=4))
-        flip_psum = ctx.enter_context(tc.psum_pool(name="flip", bufs=2))
-        mx_psum = ctx.enter_context(tc.psum_pool(name="mx", bufs=4))
-        agg_psum = ctx.enter_context(tc.psum_pool(name="agg", bufs=2))
+        rows_pool = ctx.enter_context(tc.tile_pool(name="rows", bufs=8))
+        psum = ctx.enter_context(tc.psum_pool(name="psum", bufs=8))
 
         x_nat = keep.tile([P, ROW_TILES, FEATS], BF16)
         w_raw = keep.tile([P, K_PASSES, PACK, FEATS], BF16)
@@ -113,7 +112,7 @@ def tile_module_1_pb_kernel(tc, adj, x1, W2, b2, out):
         b2_banks = []
         bn_parts = small.tile([P, HALVES], F32)
         for h in range(HALVES):
-            b2_bank = mx_psum.tile([P, BANK], F32, name="acc")
+            b2_bank = psum.tile([P, BANK], F32, tag="bank")
             nc.tensor.matmul(out=b2_bank[:], lhsT=ones[:], rhs=b2_row[:, h * BANK : (h + 1) * BANK], start=True, stop=True)
             sq_b = unread.tile([P, BANK], BF16, name="sq_s")
             nc.scalar.activation(out=sq_b[:], in_=b2_bank[:], func=ACT.Square, accum_out=bn_parts[:, h : h + 1])
@@ -148,10 +147,10 @@ def tile_module_1_pb_kernel(tc, adj, x1, W2, b2, out):
             nc.vector.quantize_mx(out=codes.bitcast(FP8X4), scales=scales, in_=grouped)
 
         def flip(words, copy_out):
-            flipped = flip_psum.tile([P, 4, P], F32)
+            flipped = psum.tile([P, 4, P], F32, tag="bank")
             for c in range(4):
                 nc.tensor.transpose(out=flipped[:, c, :], in_=words[:, c * P : (c + 1) * P], identity=ident[:])
-            grouped = stage.tile([P, 2 * P * PACK], BF16, align_bytes=64)
+            grouped = rows_pool.tile([P, 2 * P * PACK], BF16, align_bytes=64)
             copy_out(
                 out=grouped[:].bitcast(F32).rearrange("p (a r u) -> p a r u", a=2, u=2),
                 in_=flipped[:].rearrange("p (a u) r -> p a r u", u=2),
@@ -181,7 +180,7 @@ def tile_module_1_pb_kernel(tc, adj, x1, W2, b2, out):
         x_scales = keep.tile([P, ROW_TILES, K_PASSES * P], U8, align_bytes=64)
 
         def project(col, h):
-            acc = mx_psum.tile([P, BANK], F32)
+            acc = psum.tile([P, BANK], F32, tag="bank")
             for g in range(K_PASSES):
                 nc.tensor.matmul_mx(
                     out=acc[:],
@@ -208,13 +207,16 @@ def tile_module_1_pb_kernel(tc, adj, x1, W2, b2, out):
         def both(ap):
             return ap.unsqueeze(1).to_broadcast([P, 2, n])
 
+        xn = small.tile([P, ROW_TILES], F32)
+        inv_xn = small.tile([P, ROW_TILES], F32)
+        zb = small.tile([P, ROW_TILES], F32)
+
         def norms_and_codes(grp, copy_out):
-            xn_sq = single(grp, "xn_sq")
             waiting = None
             for i in range(n):
                 col = grp * n + i
                 sq_x = unread.tile([P, FEATS], BF16)
-                nc.scalar.activation(out=sq_x[:], in_=x_nat[:, col, :], func=ACT.Square, accum_out=xn_sq[:, i : i + 1])
+                nc.scalar.activation(out=sq_x[:], in_=x_nat[:, col, :], func=ACT.Square, accum_out=xn[:, col : col + 1])
                 grouped = flip(x_nat[:, col, :].bitcast(F32), copy_out)
                 if waiting is not None:
                     quantise(*waiting)
@@ -222,17 +224,15 @@ def tile_module_1_pb_kernel(tc, adj, x1, W2, b2, out):
             quantise(*waiting)
 
         def x_scalars(grp):
-            xn = scalars[grp]["xn_sq"]
-            inv_xn = single(grp, "inv_xn")
-            zb = single(grp, "zb")
-            g_one(xn[:], xn[:], MIN_NORM_SQ, ALU.max)
-            g_pow(inv_xn[:], xn[:], neg_half[:])
-            g_mul(xn[:], xn[:], inv_xn[:])
-            g_one(xn[:], xn[:], ARTANH_CLIP, ALU.min)
-            g_affine(zb[:], xn[:], 1.0, 1.0)
-            g_pow(zb[:], zb[:], neg_one[:])
-            g_affine(xn[:], xn[:], -1.0, 1.0)
-            g_mul(zb[:], zb[:], xn[:])
+            mine = slice(grp * n, (grp + 1) * n)
+            g_one(xn[:, mine], xn[:, mine], MIN_NORM_SQ, ALU.max)
+            g_pow(inv_xn[:, mine], xn[:, mine], neg_half[:])
+            g_mul(xn[:, mine], xn[:, mine], inv_xn[:, mine])
+            g_one(xn[:, mine], xn[:, mine], ARTANH_CLIP, ALU.min)
+            g_affine(zb[:, mine], xn[:, mine], 1.0, 1.0)
+            g_pow(zb[:, mine], zb[:, mine], neg_one[:])
+            g_affine(xn[:, mine], xn[:, mine], -1.0, 1.0)
+            g_mul(zb[:, mine], zb[:, mine], xn[:, mine])
 
         def sums(grp):
             mn_parts = small.tile([P, n, HALVES], F32, name="mn_parts%d" % grp)
@@ -252,6 +252,7 @@ def tile_module_1_pb_kernel(tc, adj, x1, W2, b2, out):
 
         def start_scalars(grp):
             got = scalars[grp]
+            mine = slice(grp * n, (grp + 1) * n)
             mn_e2 = double(grp, "mn_e2")
             mn, e2 = mn_e2[:, 0, :], mn_e2[:, 1, :]
             g_op(mn, got["mn_parts"][:, :, 0], got["mn_parts"][:, :, 1], ALU.add)
@@ -261,8 +262,8 @@ def tile_module_1_pb_kernel(tc, adj, x1, W2, b2, out):
             g_pow(inv_mn[:], mn, neg_half[:])
             g_mul(mn_e2[:], mn_e2[:], both(inv_mn[:]))
             z = single(grp, "z")
-            g_mul(z[:], mn, got["inv_xn"][:])
-            g_pow(z[:], got["zb"][:], z[:])
+            g_mul(z[:], mn, inv_xn[:, mine])
+            g_pow(z[:], zb[:, mine], z[:])
             p_q = double(grp, "p_q")
             p, q = p_q[:, 0, :], p_q[:, 1, :]
             g_affine(p, z[:], -1.0, 1.0)
@@ -274,32 +275,30 @@ def tile_module_1_pb_kernel(tc, adj, x1, W2, b2, out):
             g_mul(c1[:], c1[:], e2)
             times_y2 = double(grp, "times_y2")
             g_one(times_y2[:], squares[:], y2[:, 0:1], ALU.mult)
-            g_op(squares[:], squares[:], both(c1[:]), ALU.add)
+            plus_c1 = double(grp, "plus_c1")
+            g_op(plus_c1[:], squares[:], both(c1[:]), ALU.add)
             den = single(grp, "den")
-            g_op(den[:], squares[:, 1, :], times_y2[:, 0, :], ALU.add)
+            g_op(den[:], plus_c1[:, 1, :], times_y2[:, 0, :], ALU.add)
             nums = double(grp, "nums")
-            g_op(nums[:], squares[:], both(times_y2[:, 1, :]), ALU.add)
-            inv_den_q = single(grp, "inv_den_q")
-            g_mul(den[:], den[:], q)
-            g_pow(inv_den_q[:], den[:], neg_one[:])
-            inv_den = single(grp, "inv_den")
-            g_mul(inv_den[:], inv_den_q[:], q)
+            g_op(nums[:], plus_c1[:], both(times_y2[:, 1, :]), ALU.add)
+            inv_q_den_sn = single(grp, "inv_q_den_sn")
+            g_mul(den[:], den[:], nums[:, 0, :])
+            g_mul(den[:], den[:], squares[:, 1, :])
+            g_one(den[:], den[:], MIN_NORM_SQ, ALU.max)
+            g_pow(inv_q_den_sn[:], den[:], neg_half[:])
+            inv_den_sn = single(grp, "inv_den_sn")
+            g_mul(inv_den_sn[:], inv_q_den_sn[:], q)
             sn = single(grp, "sn")
-            g_mul(sn[:], nums[:, 0, :], inv_den[:])
-            g_one(sn[:], sn[:], MIN_NORM_SQ, ALU.max)
-            inv_sn = single(grp, "inv_sn")
-            g_pow(inv_sn[:], sn[:], neg_half[:])
-            g_mul(sn[:], sn[:], inv_sn[:])
+            g_mul(sn[:], nums[:, 0, :], inv_den_sn[:])
             g_one(sn[:], sn[:], MAX_NORM, ALU.min)
             log_args = double(grp, "log_args")
             g_affine(log_args[:, 0, :], sn[:], 1.0, 1.0)
             g_affine(log_args[:, 1, :], sn[:], -1.0, 1.0)
             factors = double(grp, "factors")
             g_mul(factors[:, 0, :], nums[:, 1, :], p)
-            g_mul(factors[:, 0, :], factors[:, 0, :], inv_den_q[:])
             g_mul(factors[:, 0, :], factors[:, 0, :], inv_mn[:])
-            g_mul(factors[:, 1, :], z[:], inv_den[:])
-            g_mul(factors[:], factors[:], both(inv_sn[:]))
+            g_mul(factors[:, 0, :], factors[:, 0, :], inv_q_den_sn[:])
+            g_mul(factors[:, 1, :], z[:], inv_den_sn[:])
             g_mul(factors[:], factors[:], gain_consts[:])
 
         def finish_scalars(grp):
@@ -313,36 +312,43 @@ def tile_module_1_pb_kernel(tc, adj, x1, W2, b2, out):
 
         norms_and_codes(0, nc.scalar.copy)
         x_scalars(0)
-        sums(0)
-        start_scalars(0)
         norms_and_codes(1, nc.vector.tensor_copy)
         x_scalars(1)
+        sums(0)
+        start_scalars(0)
         sums(1)
-        finish_scalars(0)
-        start_scalars(1)
 
         a_codes = keep.tile([P, GRAPHS, NODES], U32, align_bytes=64)
         a_scales = keep.tile([P, GRAPHS, NODES], U8, align_bytes=64)
-        waiting = None
-        for b in range(GRAPHS):
-            for pair in range(TILES_PER_GRAPH // 2):
-                cols = slice(pair * 2 * P, (pair + 1) * 2 * P)
-                words = a_nat[:, b, 2 * pair : 2 * pair + 2, :].rearrange("p m j -> p (m j)").bitcast(F32)
-                grouped = flip(words, nc.vector.tensor_copy)
-                if waiting is not None:
-                    quantise(*waiting)
-                waiting = (grouped[:], a_codes[:, b, cols], a_scales[:, b, cols])
-        quantise(*waiting)
+
+        def quantise_adj(copy_out):
+            waiting = None
+            for b in range(GRAPHS):
+                for pair in range(TILES_PER_GRAPH // 2):
+                    cols = slice(pair * 2 * P, (pair + 1) * 2 * P)
+                    words = a_nat[:, b, 2 * pair : 2 * pair + 2, :].rearrange("p m j -> p (m j)").bitcast(F32)
+                    grouped = flip(words, copy_out)
+                    if waiting is not None:
+                        quantise(*waiting)
+                    waiting = (grouped[:], a_codes[:, b, cols], a_scales[:, b, cols])
+            quantise(*waiting)
 
         tangent = [{} for b in range(GRAPHS)]
+
+        def spread_bias(b):
+            tangent[b]["beta_hb"] = []
+            for t in range(TILES_PER_GRAPH):
+                grp, i = divmod(b * TILES_PER_GRAPH + t, n)
+                beta_hb = bias_pool.tile([P, FEATS], F32)
+                nc.scalar.activation(out=beta_hb[:], in_=hb[:], func=ACT.Copy, scale=scalars[grp]["alpha_beta"][:, 1, i : i + 1])
+                tangent[b]["beta_hb"].append(beta_hb)
 
         def tangent_tile(b, t):
             if t == 0:
                 tangent[b]["planes"] = tan_pool.tile([P, PACK, FEATS], BF16, name="planes")
             grp, i = divmod(b * TILES_PER_GRAPH + t, n)
             alpha_beta = scalars[grp]["alpha_beta"]
-            beta_hb = bias_pool.tile([P, FEATS], F32)
-            nc.scalar.activation(out=beta_hb[:], in_=hb[:], func=ACT.Copy, scale=alpha_beta[:, 1, i : i + 1])
+            beta_hb = tangent[b]["beta_hb"][t]
             for h in range(HALVES):
                 cols = slice(h * BANK, (h + 1) * BANK)
                 acc = project(b * TILES_PER_GRAPH + t, h)
@@ -369,7 +375,7 @@ def tile_module_1_pb_kernel(tc, adj, x1, W2, b2, out):
             result = out_pool.tile([P, FEATS], F32)
             for h in range(HALVES):
                 cols = slice(h * BANK, (h + 1) * BANK)
-                agg = agg_psum.tile([P, BANK], F32)
+                agg = psum.tile([P, BANK], F32, tag="bank")
                 nc.tensor.matmul_mx(
                     out=agg[:],
                     lhsT=a_codes[:, b, m * P : (m + 1) * P].bitcast(FP8X4),
@@ -379,19 +385,30 @@ def tile_module_1_pb_kernel(tc, adj, x1, W2, b2, out):
                     start=True,
                     stop=True,
                 )
-                nc.scalar.activation(out=result[:, cols], in_=agg[:], func=ACT.Relu)
+                if b == GRAPHS - 1 and h == 1:
+                    nc.vector.tensor_scalar(out=result[:, cols], in0=agg[:], scalar1=0.0, scalar2=None, op0=ALU.max)
+                else:
+                    nc.scalar.activation(out=result[:, cols], in_=agg[:], func=ACT.Relu)
             nc.sync.dma_start(out=out[b].rearrange("(p m) f -> p m f", m=TILES_PER_GRAPH)[:, m, :], in_=result[:])
 
+        quantise_adj(nc.scalar.copy)
+        finish_scalars(0)
+        start_scalars(1)
+        spread_bias(0)
         for t in range(TILES_PER_GRAPH):
             tangent_tile(0, t)
         quantise_tangent(0)
+        spread_bias(1)
         for b in range(GRAPHS):
-            following = b + 1
-            if following == GRAPHS_PER_GROUP:
-                finish_scalars(1)
+            if b + 1 < GRAPHS:
+                tangent_tile(b + 1, 0)
             for t in range(TILES_PER_GRAPH):
-                if following < GRAPHS:
-                    tangent_tile(following, t)
+                if b + 1 < GRAPHS and t + 1 < TILES_PER_GRAPH:
+                    tangent_tile(b + 1, t + 1)
                 aggregate_tile(b, t)
-            if following < GRAPHS:
-                quantise_tangent(following)
+            if b + 1 < GRAPHS:
+                quantise_tangent(b + 1)
+            if b + 2 < GRAPHS:
+                if (b + 2) % GRAPHS_PER_GROUP == 0:
+                    finish_scalars((b + 2) // GRAPHS_PER_GROUP)
+                spread_bias(b + 2)

@@ -44,6 +44,7 @@ def tile_module_1_pb_kernel(tc, adj, x1, W2, b2, out):
         out_pool = ctx.enter_context(tc.tile_pool(name="outs", bufs=4))
         rows_pool = ctx.enter_context(tc.tile_pool(name="rows", bufs=8))
         psum = ctx.enter_context(tc.psum_pool(name="psum", bufs=8))
+        ctx.enter_context(tc.manual_schedule())
 
         x_nat = keep.tile([P, ROW_TILES, FEATS], BF16)
         w_raw = keep.tile([P, K_PASSES, PACK, FEATS], BF16)

@@ -37,12 +37,12 @@ def tile_module_1_pb_kernel(tc, adj, x1, W2, b2, out):
         const = ctx.enter_context(tc.tile_pool(name="const", bufs=1))
         keep = ctx.enter_context(tc.tile_pool(name="keep", bufs=1))
         small = ctx.enter_context(tc.tile_pool(name="small", bufs=1))
-        stage = ctx.enter_context(tc.tile_pool(name="stage", bufs=3))
+        stage = ctx.enter_context(tc.tile_pool(name="stage", bufs=2))
         unread = ctx.enter_context(tc.tile_pool(name="unread", bufs=2))
         tan_pool = ctx.enter_context(tc.tile_pool(name="tan", bufs=2))
         bias_pool = ctx.enter_context(tc.tile_pool(name="bias", bufs=4))
-        out_pool = ctx.enter_context(tc.tile_pool(name="outs", bufs=4))
-        rows_pool = ctx.enter_context(tc.tile_pool(name="rows", bufs=8))
+        out_pool = ctx.enter_context(tc.tile_pool(name="outs", bufs=6))
+        rows_pool = ctx.enter_context(tc.tile_pool(name="rows", bufs=6))
         psum = ctx.enter_context(tc.psum_pool(name="psum", bufs=8))
         ctx.enter_context(tc.manual_schedule())
 
@@ -322,9 +322,9 @@ def tile_module_1_pb_kernel(tc, adj, x1, W2, b2, out):
         a_codes = keep.tile([P, GRAPHS, NODES], U32, align_bytes=64)
         a_scales = keep.tile([P, GRAPHS, NODES], U8, align_bytes=64)
 
-        def quantise_adj(copy_out):
+        def quantise_adj(graphs, copy_out):
             waiting = None
-            for b in range(GRAPHS):
+            for b in graphs:
                 for pair in range(TILES_PER_GRAPH // 2):
                     cols = slice(pair * 2 * P, (pair + 1) * 2 * P)
                     words = a_nat[:, b, 2 * pair : 2 * pair + 2, :].rearrange("p m j -> p (m j)").bitcast(F32)
@@ -392,12 +392,13 @@ def tile_module_1_pb_kernel(tc, adj, x1, W2, b2, out):
                     nc.scalar.activation(out=result[:, cols], in_=agg[:], func=ACT.Relu)
             nc.sync.dma_start(out=out[b].rearrange("(p m) f -> p m f", m=TILES_PER_GRAPH)[:, m, :], in_=result[:])
 
-        quantise_adj(nc.scalar.copy)
+        quantise_adj([0, 1], nc.vector.tensor_copy)
         finish_scalars(0)
         start_scalars(1)
         spread_bias(0)
         for t in range(TILES_PER_GRAPH):
             tangent_tile(0, t)
+        quantise_adj([2, 3], nc.scalar.copy)
         quantise_tangent(0)
         spread_bias(1)
         for b in range(GRAPHS):

@@ -37,12 +37,12 @@ def tile_module_1_pb_kernel(tc, adj, x1, W2, b2, out):
         const = ctx.enter_context(tc.tile_pool(name="const", bufs=1))
         keep = ctx.enter_context(tc.tile_pool(name="keep", bufs=1))
         small = ctx.enter_context(tc.tile_pool(name="small", bufs=1))
-        stage = ctx.enter_context(tc.tile_pool(name="stage", bufs=2))
+        stage = ctx.enter_context(tc.tile_pool(name="stage", bufs=3))
         unread = ctx.enter_context(tc.tile_pool(name="unread", bufs=2))
         tan_pool = ctx.enter_context(tc.tile_pool(name="tan", bufs=2))
         bias_pool = ctx.enter_context(tc.tile_pool(name="bias", bufs=4))
-        out_pool = ctx.enter_context(tc.tile_pool(name="outs", bufs=6))
-        rows_pool = ctx.enter_context(tc.tile_pool(name="rows", bufs=6))
+        out_pool = ctx.enter_context(tc.tile_pool(name="outs", bufs=4))
+        rows_pool = ctx.enter_context(tc.tile_pool(name="rows", bufs=8))
         psum = ctx.enter_context(tc.psum_pool(name="psum", bufs=8))
         ctx.enter_context(tc.manual_schedule())
 
@@ -81,6 +81,8 @@ def tile_module_1_pb_kernel(tc, adj, x1, W2, b2, out):
 
         ones = const.tile([P, P], BF16)
         nc.vector.memset(ones[:], 1.0)
+        one = const.tile([P, 1], F32)
+        nc.vector.memset(one[:], 1.0)
         one_half = const.tile([P, 1], F32)
         nc.gpsimd.memset(one_half[:], 0.5)
         ident = const.tile([P, P], F32)
@@ -89,9 +91,6 @@ def tile_module_1_pb_kernel(tc, adj, x1, W2, b2, out):
         nc.gpsimd.memset(neg_half[:], -0.5)
         neg_one = const.tile([P, GROUP_TILES], F32)
         nc.gpsimd.memset(neg_one[:], -1.0)
-        gain_consts = const.tile([P, 2, GROUP_TILES], F32)
-        nc.gpsimd.memset(gain_consts[:, 0, :], 0.5)
-        nc.gpsimd.memset(gain_consts[:, 1, :], 2.0)
         warm = const.tile([P, 1], F32)
         nc.scalar.activation(out=warm[:], in_=one_half[:], func=ACT.Ln)
 
@@ -251,6 +250,12 @@ def tile_module_1_pb_kernel(tc, adj, x1, W2, b2, out):
                     sq_s = unread.tile([P, BANK], BF16)
                     nc.scalar.activation(out=sq_s[:], in_=acc[:], func=ACT.Square, accum_out=mn_parts[:, i, h : h + 1])
 
+        def v_mul(o, a, b):
+            nc.vector.tensor_tensor(out=o, in0=a, in1=b, op=ALU.mult)
+
+        def v_two(o, a, scalar, b):
+            nc.vector.scalar_tensor_tensor(out=o, in0=a, scalar=scalar, in1=b, op0=ALU.mult, op1=ALU.mult)
+
         def start_scalars(grp):
             got = scalars[grp]
             mine = slice(grp * n, (grp + 1) * n)
@@ -287,29 +292,26 @@ def tile_module_1_pb_kernel(tc, adj, x1, W2, b2, out):
             g_mul(den[:], den[:], squares[:, 1, :])
             g_one(den[:], den[:], MIN_NORM_SQ, ALU.max)
             g_pow(inv_q_den_sn[:], den[:], neg_half[:])
-            inv_den_sn = single(grp, "inv_den_sn")
-            g_mul(inv_den_sn[:], inv_q_den_sn[:], q)
-            sn = single(grp, "sn")
-            g_mul(sn[:], nums[:, 0, :], inv_den_sn[:])
-            g_one(sn[:], sn[:], MAX_NORM, ALU.min)
-            log_args = double(grp, "log_args")
-            g_affine(log_args[:, 0, :], sn[:], 1.0, 1.0)
-            g_affine(log_args[:, 1, :], sn[:], -1.0, 1.0)
-            factors = double(grp, "factors")
-            g_mul(factors[:, 0, :], nums[:, 1, :], p)
-            g_mul(factors[:, 0, :], factors[:, 0, :], inv_mn[:])
-            g_mul(factors[:, 0, :], factors[:, 0, :], inv_q_den_sn[:])
-            g_mul(factors[:, 1, :], z[:], inv_den_sn[:])
-            g_mul(factors[:], factors[:], gain_consts[:])
 
         def finish_scalars(grp):
             got = scalars[grp]
+            inv_den_sn = single(grp, "inv_den_sn")
+            v_mul(inv_den_sn[:], got["inv_q_den_sn"][:], got["p_q"][:, 1, :])
+            sn = single(grp, "sn")
+            v_mul(sn[:], got["nums"][:, 0, :], inv_den_sn[:])
+            nc.vector.tensor_scalar(out=sn[:], in0=sn[:], scalar1=MAX_NORM, scalar2=None, op0=ALU.min)
             logs = double(grp, "logs")
-            nc.scalar.activation(out=logs[:], in_=got["log_args"][:], func=ACT.Ln)
-            log_ratio = single(grp, "log_ratio")
-            g_op(log_ratio[:], logs[:, 0, :], logs[:, 1, :], ALU.subtract)
+            nc.scalar.activation(out=logs[:, 0, :], in_=sn[:], func=ACT.Ln, scale=1.0, bias=one[:, 0:1])
+            nc.scalar.activation(out=logs[:, 1, :], in_=sn[:], func=ACT.Ln, scale=-1.0, bias=one[:, 0:1])
             alpha_beta = double(grp, "alpha_beta")
-            g_mul(alpha_beta[:], got["factors"][:], both(log_ratio[:]))
+            alpha, beta = alpha_beta[:, 0, :], alpha_beta[:, 1, :]
+            v_two(alpha, got["nums"][:, 1, :], 0.5, got["p_q"][:, 0, :])
+            v_two(beta, got["z"][:], 2.0, inv_den_sn[:])
+            v_mul(alpha, alpha, got["inv_mn"][:])
+            v_mul(alpha, alpha, got["inv_q_den_sn"][:])
+            log_ratio = single(grp, "log_ratio")
+            nc.vector.tensor_tensor(out=log_ratio[:], in0=logs[:, 0, :], in1=logs[:, 1, :], op=ALU.subtract)
+            v_mul(alpha_beta[:], alpha_beta[:], both(log_ratio[:]))
 
         norms_and_codes(0, nc.scalar.copy)
         x_scalars(0)
@@ -318,13 +320,14 @@ def tile_module_1_pb_kernel(tc, adj, x1, W2, b2, out):
         sums(0)
         start_scalars(0)
         sums(1)
+        start_scalars(1)
 
         a_codes = keep.tile([P, GRAPHS, NODES], U32, align_bytes=64)
         a_scales = keep.tile([P, GRAPHS, NODES], U8, align_bytes=64)
 
-        def quantise_adj(graphs, copy_out):
+        def quantise_adj(copy_out):
             waiting = None
-            for b in graphs:
+            for b in range(GRAPHS):
                 for pair in range(TILES_PER_GRAPH // 2):
                     cols = slice(pair * 2 * P, (pair + 1) * 2 * P)
                     words = a_nat[:, b, 2 * pair : 2 * pair + 2, :].rearrange("p m j -> p (m j)").bitcast(F32)
@@ -392,13 +395,11 @@ def tile_module_1_pb_kernel(tc, adj, x1, W2, b2, out):
                     nc.scalar.activation(out=result[:, cols], in_=agg[:], func=ACT.Relu)
             nc.sync.dma_start(out=out[b].rearrange("(p m) f -> p m f", m=TILES_PER_GRAPH)[:, m, :], in_=result[:])
 
-        quantise_adj([0, 1], nc.vector.tensor_copy)
+        quantise_adj(nc.scalar.copy)
         finish_scalars(0)
-        start_scalars(1)
         spread_bias(0)
         for t in range(TILES_PER_GRAPH):
             tangent_tile(0, t)
-        quantise_adj([2, 3], nc.scalar.copy)
         quantise_tangent(0)
         spread_bias(1)
         for b in range(GRAPHS):
@@ -408,9 +409,9 @@ def tile_module_1_pb_kernel(tc, adj, x1, W2, b2, out):
                 if b + 1 < GRAPHS and t + 1 < TILES_PER_GRAPH:
                     tangent_tile(b + 1, t + 1)
                 aggregate_tile(b, t)
+            if b + 2 < GRAPHS and (b + 2) % GRAPHS_PER_GROUP == 0:
+                finish_scalars((b + 2) // GRAPHS_PER_GROUP)
             if b + 1 < GRAPHS:
                 quantise_tangent(b + 1)
             if b + 2 < GRAPHS:
-                if (b + 2) % GRAPHS_PER_GROUP == 0:
-                    finish_scalars((b + 2) // GRAPHS_PER_GROUP)
                 spread_bias(b + 2)

@@ -293,7 +293,7 @@ def tile_module_1_pb_kernel(tc, adj, x1, W2, b2, out):
             g_one(den[:], den[:], MIN_NORM_SQ, ALU.max)
             g_pow(inv_q_den_sn[:], den[:], neg_half[:])
 
-        def finish_scalars(grp):
+        def take_logs(grp):
             got = scalars[grp]
             inv_den_sn = single(grp, "inv_den_sn")
             v_mul(inv_den_sn[:], got["inv_q_den_sn"][:], got["p_q"][:, 1, :])
@@ -303,6 +303,11 @@ def tile_module_1_pb_kernel(tc, adj, x1, W2, b2, out):
             logs = double(grp, "logs")
             nc.scalar.activation(out=logs[:, 0, :], in_=sn[:], func=ACT.Ln, scale=1.0, bias=one[:, 0:1])
             nc.scalar.activation(out=logs[:, 1, :], in_=sn[:], func=ACT.Ln, scale=-1.0, bias=one[:, 0:1])
+
+        def finish_scalars(grp):
+            got = scalars[grp]
+            logs = got["logs"]
+            inv_den_sn = got["inv_den_sn"]
             alpha_beta = double(grp, "alpha_beta")
             alpha, beta = alpha_beta[:, 0, :], alpha_beta[:, 1, :]
             v_two(alpha, got["nums"][:, 1, :], 0.5, got["p_q"][:, 0, :])
@@ -331,7 +336,7 @@ def tile_module_1_pb_kernel(tc, adj, x1, W2, b2, out):
                 for pair in range(TILES_PER_GRAPH // 2):
                     cols = slice(pair * 2 * P, (pair + 1) * 2 * P)
                     words = a_nat[:, b, 2 * pair : 2 * pair + 2, :].rearrange("p m j -> p (m j)").bitcast(F32)
-                    grouped = flip(words, copy_out)
+                    grouped = flip(words, nc.vector.tensor_copy if b < GRAPHS_PER_GROUP else nc.scalar.copy)
                     if waiting is not None:
                         quantise(*waiting)
                     waiting = (grouped[:], a_codes[:, b, cols], a_scales[:, b, cols])
@@ -396,6 +401,7 @@ def tile_module_1_pb_kernel(tc, adj, x1, W2, b2, out):
             nc.sync.dma_start(out=out[b].rearrange("(p m) f -> p m f", m=TILES_PER_GRAPH)[:, m, :], in_=result[:])
 
         quantise_adj(nc.scalar.copy)
+        take_logs(0)
         finish_scalars(0)
         spread_bias(0)
         for t in range(TILES_PER_GRAPH):
@@ -408,6 +414,8 @@ def tile_module_1_pb_kernel(tc, adj, x1, W2, b2, out):
             for t in range(TILES_PER_GRAPH):
                 if b + 1 < GRAPHS and t + 1 < TILES_PER_GRAPH:
                     tangent_tile(b + 1, t + 1)
+                if b + 2 == GRAPHS_PER_GROUP and t == TILES_PER_GRAPH - 1:
+                    take_logs(1)
                 aggregate_tile(b, t)
             if b + 2 < GRAPHS and (b + 2) % GRAPHS_PER_GROUP == 0:
                 finish_scalars((b + 2) // GRAPHS_PER_GROUP)

@@ -20,13 +20,15 @@ TILES_PER_GRAPH = NODES // P
 ROW_TILES = GRAPHS * TILES_PER_GRAPH
 K_PASSES = FEATS // (P * PACK)
 HALVES = FEATS // BANK
-GROUPS = 2
-GROUP_TILES = ROW_TILES // GROUPS
-GRAPHS_PER_GROUP = GRAPHS // GROUPS
+GROUP_TILES = (8, 8)
+GROUP_FIRST = (0, 8)
+GROUPS = len(GROUP_TILES)
+GROUP_OF = [grp for grp in range(GROUPS) for i in range(GROUP_TILES[grp])]
 
 MIN_NORM_SQ = 1e-30
 MAX_NORM = 0.996
 ARTANH_CLIP = 1.0 - 1e-7
+TINY = 2.0**-100
 
 FLOPS = 2 * GRAPHS * NODES * FEATS * FEATS + 2 * GRAPHS * NODES * NODES * FEATS
 
@@ -37,10 +39,11 @@ def tile_module_1_pb_kernel(tc, adj, x1, W2, b2, out):
         const = ctx.enter_context(tc.tile_pool(name="const", bufs=1))
         keep = ctx.enter_context(tc.tile_pool(name="keep", bufs=1))
         small = ctx.enter_context(tc.tile_pool(name="small", bufs=1))
-        stage = ctx.enter_context(tc.tile_pool(name="stage", bufs=3))
+        stage = ctx.enter_context(tc.tile_pool(name="stage", bufs=2))
         unread = ctx.enter_context(tc.tile_pool(name="unread", bufs=2))
-        tan_pool = ctx.enter_context(tc.tile_pool(name="tan", bufs=2))
-        bias_pool = ctx.enter_context(tc.tile_pool(name="bias", bufs=4))
+        tan_pool = ctx.enter_context(tc.tile_pool(name="tan", bufs=3))
+        planes_pool = ctx.enter_context(tc.tile_pool(name="planes", bufs=5))
+        bias_pool = ctx.enter_context(tc.tile_pool(name="bias", bufs=16))
         out_pool = ctx.enter_context(tc.tile_pool(name="outs", bufs=4))
         rows_pool = ctx.enter_context(tc.tile_pool(name="rows", bufs=8))
         psum = ctx.enter_context(tc.psum_pool(name="psum", bufs=8))
@@ -50,11 +53,11 @@ def tile_module_1_pb_kernel(tc, adj, x1, W2, b2, out):
         w_raw = keep.tile([P, K_PASSES, PACK, FEATS], BF16)
         a_nat = keep.tile([P, GRAPHS, TILES_PER_GRAPH, NODES], BF16)
 
-        def load_x(b):
-            cols = slice(b * TILES_PER_GRAPH, (b + 1) * TILES_PER_GRAPH)
+        def load_x(b, u):
+            first = b * TILES_PER_GRAPH + 2 * u
             nc.sync.dma_start(
-                out=x_nat[:, cols, :].rearrange("p (u e) k -> p u (e k)", e=2),
-                in_=x1[b].rearrange("(u p e) k -> p u (e k)", u=2, e=2),
+                out=x_nat[:, first : first + 2, :].rearrange("p e k -> p (e k)"),
+                in_=x1[b][2 * P * u : 2 * P * (u + 1), :].rearrange("(p e) k -> p (e k)", e=2),
             )
 
         def load_w(g):
@@ -65,14 +68,16 @@ def tile_module_1_pb_kernel(tc, adj, x1, W2, b2, out):
             )
 
         b2_row = const.tile([P, FEATS], BF16)
-        nc.vector.memset(b2_row[:], 0.0)
+        nc.vector.memset(b2_row[:, 0:BANK], 0.0)
+        nc.gpsimd.memset(b2_row[:, BANK:FEATS], 0.0)
+        load_x(0, 0)
         nc.sync.dma_start(out=b2_row[0:1, :], in_=b2.rearrange("(o h) -> o h", o=1))
-        load_x(0)
         load_w(0)
+        load_x(0, 1)
         load_w(1)
-        load_x(1)
-        load_x(2)
-        load_x(3)
+        for b in range(1, GRAPHS):
+            load_x(b, 0)
+            load_x(b, 1)
         for b in range(GRAPHS):
             nc.sync.dma_start(
                 out=a_nat[:, b, :, :].rearrange("p m j -> p (m j)"),
@@ -87,9 +92,9 @@ def tile_module_1_pb_kernel(tc, adj, x1, W2, b2, out):
         nc.gpsimd.memset(one_half[:], 0.5)
         ident = const.tile([P, P], F32)
         make_identity(nc, ident[:])
-        neg_half = const.tile([P, GROUP_TILES], F32)
+        neg_half = const.tile([P, ROW_TILES], F32)
         nc.gpsimd.memset(neg_half[:], -0.5)
-        neg_one = const.tile([P, GROUP_TILES], F32)
+        neg_one = const.tile([P, ROW_TILES], F32)
         nc.gpsimd.memset(neg_one[:], -1.0)
         warm = const.tile([P, 1], F32)
         nc.scalar.activation(out=warm[:], in_=one_half[:], func=ACT.Ln)
@@ -109,33 +114,38 @@ def tile_module_1_pb_kernel(tc, adj, x1, W2, b2, out):
         def g_one(o, a, scalar, op):
             nc.gpsimd.tensor_scalar(out=o, in0=a, scalar1=scalar, scalar2=None, op0=op)
 
-        b2_banks = []
+        b2_all = const.tile([P, FEATS], F32)
         bn_parts = small.tile([P, HALVES], F32)
         for h in range(HALVES):
             b2_bank = psum.tile([P, BANK], F32, tag="bank")
-            nc.tensor.matmul(out=b2_bank[:], lhsT=ones[:], rhs=b2_row[:, h * BANK : (h + 1) * BANK], start=True, stop=True)
+            cols = slice(h * BANK, (h + 1) * BANK)
+            nc.tensor.matmul(out=b2_bank[:], lhsT=ones[:], rhs=b2_row[:, cols], start=True, stop=True)
             sq_b = unread.tile([P, BANK], BF16, name="sq_s")
             nc.scalar.activation(out=sq_b[:], in_=b2_bank[:], func=ACT.Square, accum_out=bn_parts[:, h : h + 1])
-            b2_banks.append(b2_bank)
+            nc.vector.tensor_copy(out=b2_all[:, cols], in_=b2_bank[:])
         bn = small.tile([P, 1], F32)
         inv_bn = small.tile([P, 1], F32)
         decay = small.tile([P, 1], F32)
         hb_norm = small.tile([P, 1], F32)
         hb_scale = small.tile([P, 1], F32)
+        two_hb_scale = small.tile([P, 1], F32)
         y2 = small.tile([P, 1], F32)
-        g_op(bn[:], bn_parts[:, 0:1], bn_parts[:, 1:2], ALU.add)
-        g_one(bn[:], bn[:], MIN_NORM_SQ, ALU.max)
-        g_pow(inv_bn[:], bn[:], neg_half[:, 0:1])
-        g_mul(bn[:], bn[:], inv_bn[:])
-        g_one(bn[:], bn[:], 2.0 / math.log(2.0), ALU.mult)
-        g_pow(decay[:], one_half[:], bn[:])
-        g_affine(hb_norm[:], decay[:], 1.0, 1.0)
-        g_pow(hb_norm[:], hb_norm[:], neg_one[:, 0:1])
-        g_affine(decay[:], decay[:], -1.0, 1.0)
-        g_mul(hb_norm[:], hb_norm[:], decay[:])
-        g_one(hb_norm[:], hb_norm[:], MAX_NORM, ALU.min)
-        g_mul(hb_scale[:], hb_norm[:], inv_bn[:])
-        g_mul(y2[:], hb_norm[:], hb_norm[:])
+
+        def bias_scalars():
+            g_op(bn[:], bn_parts[:, 0:1], bn_parts[:, 1:2], ALU.add)
+            g_one(bn[:], bn[:], MIN_NORM_SQ, ALU.max)
+            g_pow(inv_bn[:], bn[:], neg_half[:, 0:1])
+            g_mul(bn[:], bn[:], inv_bn[:])
+            g_one(bn[:], bn[:], 2.0 / math.log(2.0), ALU.mult)
+            g_pow(decay[:], one_half[:], bn[:])
+            g_affine(hb_norm[:], decay[:], 1.0, 1.0)
+            g_pow(hb_norm[:], hb_norm[:], neg_one[:, 0:1])
+            g_affine(decay[:], decay[:], -1.0, 1.0)
+            g_mul(hb_norm[:], hb_norm[:], decay[:])
+            g_one(hb_norm[:], hb_norm[:], MAX_NORM, ALU.min)
+            g_mul(hb_scale[:], hb_norm[:], inv_bn[:])
+            g_one(two_hb_scale[:], hb_scale[:], 2.0, ALU.mult)
+            g_mul(y2[:], hb_norm[:], hb_norm[:])
 
         def regroup(dst, src):
             nc.vector.tensor_copy(
@@ -159,96 +169,116 @@ def tile_module_1_pb_kernel(tc, adj, x1, W2, b2, out):
 
         w_codes = keep.tile([P, K_PASSES, FEATS], U32, align_bytes=64)
         w_scales = keep.tile([P, K_PASSES, FEATS], U8, align_bytes=64)
-        waiting = None
-        for h in range(HALVES):
-            for g in range(K_PASSES):
-                cols = slice(h * BANK, (h + 1) * BANK)
-                w_grouped = stage.tile([P, BANK, PACK], BF16, align_bytes=64)
-                regroup(w_grouped[:], w_raw[:, g, :, cols])
-                if waiting is not None:
-                    quantise(*waiting)
-                waiting = (w_grouped[:].rearrange("p c t -> p (c t)"), w_codes[:, g, cols], w_scales[:, g, cols])
-        quantise(*waiting)
+        w_grouped = {}
 
-        hb = const.tile([P, FEATS], F32)
-        for h in range(HALVES):
-            nc.vector.tensor_scalar(
-                out=hb[:, h * BANK : (h + 1) * BANK], in0=b2_banks[h][:], scalar1=hb_scale[:, 0:1], scalar2=None, op0=ALU.mult
-            )
+        def group_w(g, h):
+            w_grouped[g, h] = stage.tile([P, BANK, PACK], BF16, align_bytes=64, name="w_grouped")
+            regroup(w_grouped[g, h][:], w_raw[:, g, :, h * BANK : (h + 1) * BANK])
+
+        def quantise_w(g, h):
+            cols = slice(h * BANK, (h + 1) * BANK)
+            quantise(w_grouped[g, h][:].rearrange("p c t -> p (c t)"), w_codes[:, g, cols], w_scales[:, g, cols])
 
         x_codes = keep.tile([P, ROW_TILES, K_PASSES * P], U32, align_bytes=64)
         x_scales = keep.tile([P, ROW_TILES, K_PASSES * P], U8, align_bytes=64)
 
-        def project(col, h):
+        def project(col, first, width):
             acc = psum.tile([P, BANK], F32, tag="bank")
+            cols = slice(first, first + width)
             for g in range(K_PASSES):
                 nc.tensor.matmul_mx(
-                    out=acc[:],
+                    out=acc[:, 0:width],
                     lhsT=x_codes[:, col, g * P : (g + 1) * P].bitcast(FP8X4),
                     lhsT_scale=x_scales[:, col, g * P : (g + 1) * P],
-                    rhs=w_codes[:, g, h * BANK : (h + 1) * BANK].bitcast(FP8X4),
-                    rhs_scale=w_scales[:, g, h * BANK : (h + 1) * BANK],
+                    rhs=w_codes[:, g, cols].bitcast(FP8X4),
+                    rhs_scale=w_scales[:, g, cols],
                     start=(g == 0),
                     stop=(g == K_PASSES - 1),
                 )
             return acc
 
-        n = GROUP_TILES
+        def locate(col):
+            grp = GROUP_OF[col]
+            return grp, col - GROUP_FIRST[grp]
+
         scalars = [{} for grp in range(GROUPS)]
 
         def single(grp, label):
-            scalars[grp][label] = small.tile([P, n], F32, name="%s%d" % (label, grp))
+            scalars[grp][label] = small.tile([P, GROUP_TILES[grp]], F32, name="%s%d" % (label, grp))
             return scalars[grp][label]
 
         def double(grp, label):
-            scalars[grp][label] = small.tile([P, 2, n], F32, name="%s%d" % (label, grp))
+            scalars[grp][label] = small.tile([P, 2, GROUP_TILES[grp]], F32, name="%s%d" % (label, grp))
             return scalars[grp][label]
 
         def both(ap):
-            return ap.unsqueeze(1).to_broadcast([P, 2, n])
+            return ap.unsqueeze(1).to_broadcast([P, 2, ap.shape[1]])
 
         xn = small.tile([P, ROW_TILES], F32)
         inv_xn = small.tile([P, ROW_TILES], F32)
         zb = small.tile([P, ROW_TILES], F32)
+        one_plus = small.tile([P, ROW_TILES], F32)
 
-        def norms_and_codes(grp, copy_out):
-            waiting = None
-            for i in range(n):
-                col = grp * n + i
-                sq_x = unread.tile([P, FEATS], BF16)
-                nc.scalar.activation(out=sq_x[:], in_=x_nat[:, col, :], func=ACT.Square, accum_out=xn[:, col : col + 1])
-                grouped = flip(x_nat[:, col, :].bitcast(F32), copy_out)
-                if waiting is not None:
-                    quantise(*waiting)
-                waiting = (grouped[:], x_codes[:, col, :], x_scales[:, col, :])
-            quantise(*waiting)
+        x_grouped = {}
+
+        def square_x(col):
+            sq_x = unread.tile([P, FEATS], BF16)
+            nc.scalar.activation(out=sq_x[:], in_=x_nat[:, col, :], func=ACT.Square, accum_out=xn[:, col : col + 1])
+
+        def flip_x(col, copy_out):
+            x_grouped[col] = flip(x_nat[:, col, :].bitcast(F32), copy_out)
+
+        def gram_x(col):
+            gram = psum.tile([P, BANK], F32, tag="bank")
+            chunks = x_grouped[col][:].rearrange("p (a r t) -> p a t r", a=K_PASSES, t=PACK)
+            for c in range(K_PASSES * PACK):
+                a, t = divmod(c, PACK)
+                nc.tensor.matmul(
+                    out=gram[:, 0:P], lhsT=chunks[:, a, t, :], rhs=chunks[:, a, t, :],
+                    start=(c == 0), stop=(c == K_PASSES * PACK - 1),
+                )
+            return gram
+
+        def diagonal(col, gram):
+            picked = unread.tile([P, P], F32)
+            nc.vector.scalar_tensor_tensor(
+                out=picked[:], in0=gram[:, 0:P], scalar=1.0, in1=ident[:],
+                op0=ALU.mult, op1=ALU.mult, accum_out=xn[:, col : col + 1],
+            )
+
+        def quantise_x(col):
+            quantise(x_grouped[col][:], x_codes[:, col, :], x_scales[:, col, :])
+
+        def v_op(o, a, b, op):
+            nc.vector.tensor_tensor(out=o, in0=a, in1=b, op=op)
 
         def x_scalars(grp):
-            mine = slice(grp * n, (grp + 1) * n)
-            g_one(xn[:, mine], xn[:, mine], MIN_NORM_SQ, ALU.max)
-            g_pow(inv_xn[:, mine], xn[:, mine], neg_half[:])
+            n = GROUP_TILES[grp]
+            mine = slice(GROUP_FIRST[grp], GROUP_FIRST[grp] + n)
+            g_one(xn[:, mine], xn[:, mine], TINY, ALU.max)
+            g_pow(inv_xn[:, mine], xn[:, mine], neg_half[:, 0:n])
             g_mul(xn[:, mine], xn[:, mine], inv_xn[:, mine])
-            g_one(xn[:, mine], xn[:, mine], ARTANH_CLIP, ALU.min)
-            g_affine(zb[:, mine], xn[:, mine], 1.0, 1.0)
-            g_pow(zb[:, mine], zb[:, mine], neg_one[:])
-            g_affine(xn[:, mine], xn[:, mine], -1.0, 1.0)
-            g_mul(zb[:, mine], zb[:, mine], xn[:, mine])
+            g_one(zb[:, mine], xn[:, mine], ARTANH_CLIP, ALU.min)
+            g_affine(one_plus[:, mine], zb[:, mine], 1.0, 1.0)
+            g_affine(zb[:, mine], zb[:, mine], -1.0, 1.0)
+            g_pow(one_plus[:, mine], one_plus[:, mine], neg_one[:, 0:n])
+            g_mul(zb[:, mine], zb[:, mine], one_plus[:, mine])
 
-        def sums(grp):
-            mn_parts = small.tile([P, n, HALVES], F32, name="mn_parts%d" % grp)
-            dot_parts = small.tile([P, n, HALVES], F32, name="dot_parts%d" % grp)
-            scalars[grp]["mn_parts"] = mn_parts
-            scalars[grp]["dot_parts"] = dot_parts
-            for i in range(n):
-                for h in range(HALVES):
-                    acc = project(grp * n + i, h)
-                    prod_v = unread.tile([P, BANK], F32)
-                    nc.vector.scalar_tensor_tensor(
-                        out=prod_v[:], in0=acc[:], scalar=2.0, in1=hb[:, h * BANK : (h + 1) * BANK],
-                        op0=ALU.mult, op1=ALU.mult, accum_out=dot_parts[:, i, h : h + 1],
-                    )
-                    sq_s = unread.tile([P, BANK], BF16)
-                    nc.scalar.activation(out=sq_s[:], in_=acc[:], func=ACT.Square, accum_out=mn_parts[:, i, h : h + 1])
+        for grp in range(GROUPS):
+            scalars[grp]["parts"] = small.tile([P, HALVES, 2, GROUP_TILES[grp]], F32, name="parts%d" % grp)
+
+        def dot_hb(col, h, acc):
+            grp, i = locate(col)
+            prod_v = unread.tile([P, BANK], F32)
+            nc.vector.scalar_tensor_tensor(
+                out=prod_v[:], in0=acc[:], scalar=2.0, in1=b2_all[:, h * BANK : (h + 1) * BANK],
+                op0=ALU.mult, op1=ALU.mult, accum_out=scalars[grp]["parts"][:, h, 1, i : i + 1],
+            )
+
+        def square_mx(col, h, acc):
+            grp, i = locate(col)
+            sq_s = unread.tile([P, BANK], BF16)
+            nc.scalar.activation(out=sq_s[:], in_=acc[:], func=ACT.Square, accum_out=scalars[grp]["parts"][:, h, 0, i : i + 1])
 
         def v_mul(o, a, b):
             nc.vector.tensor_tensor(out=o, in0=a, in1=b, op=ALU.mult)
@@ -256,17 +286,20 @@ def tile_module_1_pb_kernel(tc, adj, x1, W2, b2, out):
         def v_two(o, a, scalar, b):
             nc.vector.scalar_tensor_tensor(out=o, in0=a, scalar=scalar, in1=b, op0=ALU.mult, op1=ALU.mult)
 
+        def norm_mx(grp):
+            parts = scalars[grp]["parts"]
+            mn_e2 = double(grp, "mn_e2")
+            g_op(mn_e2[:], parts[:, 0], parts[:, 1], ALU.add)
+
         def start_scalars(grp):
             got = scalars[grp]
-            mine = slice(grp * n, (grp + 1) * n)
-            mn_e2 = double(grp, "mn_e2")
-            mn, e2 = mn_e2[:, 0, :], mn_e2[:, 1, :]
-            g_op(mn, got["mn_parts"][:, :, 0], got["mn_parts"][:, :, 1], ALU.add)
-            g_op(e2, got["dot_parts"][:, :, 0], got["dot_parts"][:, :, 1], ALU.add)
-            g_one(mn, mn, MIN_NORM_SQ, ALU.max)
+            n = GROUP_TILES[grp]
+            mine = slice(GROUP_FIRST[grp], GROUP_FIRST[grp] + n)
+            mn, e2 = got["mn_e2"][:, 0, :], got["mn_e2"][:, 1, :]
             inv_mn = single(grp, "inv_mn")
-            g_pow(inv_mn[:], mn, neg_half[:])
-            g_mul(mn_e2[:], mn_e2[:], both(inv_mn[:]))
+            g_one(mn, mn, TINY, ALU.max)
+            g_pow(inv_mn[:], mn, neg_half[:, 0:n])
+            g_mul(mn, mn, inv_mn[:])
             z = single(grp, "z")
             g_mul(z[:], mn, inv_xn[:, mine])
             g_pow(z[:], zb[:, mine], z[:])
@@ -278,6 +311,8 @@ def tile_module_1_pb_kernel(tc, adj, x1, W2, b2, out):
             g_mul(squares[:], p_q[:], p_q[:])
             c1 = single(grp, "c1")
             g_mul(c1[:], p, q)
+            g_mul(e2, e2, inv_mn[:])
+            g_one(e2, e2, hb_scale[:, 0:1], ALU.mult)
             g_mul(c1[:], c1[:], e2)
             times_y2 = double(grp, "times_y2")
             g_one(times_y2[:], squares[:], y2[:, 0:1], ALU.mult)
@@ -287,139 +322,226 @@ def tile_module_1_pb_kernel(tc, adj, x1, W2, b2, out):
             g_op(den[:], plus_c1[:, 1, :], times_y2[:, 0, :], ALU.add)
             nums = double(grp, "nums")
             g_op(nums[:], plus_c1[:], both(times_y2[:, 1, :]), ALU.add)
-            inv_q_den_sn = single(grp, "inv_q_den_sn")
             g_mul(den[:], den[:], nums[:, 0, :])
             g_mul(den[:], den[:], squares[:, 1, :])
-            g_one(den[:], den[:], MIN_NORM_SQ, ALU.max)
-            g_pow(inv_q_den_sn[:], den[:], neg_half[:])
 
-        def take_logs(grp):
+        def root_scalars(grp):
+            got = scalars[grp]
+            n = GROUP_TILES[grp]
+            den = got["den"]
+            inv_q_den_sn = single(grp, "inv_q_den_sn")
+            g_one(den[:], den[:], TINY, ALU.max)
+            g_pow(inv_q_den_sn[:], den[:], neg_half[:, 0:n])
+
+        def late_ops(grp):
             got = scalars[grp]
             inv_den_sn = single(grp, "inv_den_sn")
-            v_mul(inv_den_sn[:], got["inv_q_den_sn"][:], got["p_q"][:, 1, :])
             sn = single(grp, "sn")
-            v_mul(sn[:], got["nums"][:, 0, :], inv_den_sn[:])
-            nc.vector.tensor_scalar(out=sn[:], in0=sn[:], scalar1=MAX_NORM, scalar2=None, op0=ALU.min)
             logs = double(grp, "logs")
-            nc.scalar.activation(out=logs[:, 0, :], in_=sn[:], func=ACT.Ln, scale=1.0, bias=one[:, 0:1])
-            nc.scalar.activation(out=logs[:, 1, :], in_=sn[:], func=ACT.Ln, scale=-1.0, bias=one[:, 0:1])
-
-        def finish_scalars(grp):
-            got = scalars[grp]
-            logs = got["logs"]
-            inv_den_sn = got["inv_den_sn"]
             alpha_beta = double(grp, "alpha_beta")
             alpha, beta = alpha_beta[:, 0, :], alpha_beta[:, 1, :]
-            v_two(alpha, got["nums"][:, 1, :], 0.5, got["p_q"][:, 0, :])
-            v_two(beta, got["z"][:], 2.0, inv_den_sn[:])
-            v_mul(alpha, alpha, got["inv_mn"][:])
-            v_mul(alpha, alpha, got["inv_q_den_sn"][:])
             log_ratio = single(grp, "log_ratio")
-            nc.vector.tensor_tensor(out=log_ratio[:], in0=logs[:, 0, :], in1=logs[:, 1, :], op=ALU.subtract)
-            v_mul(alpha_beta[:], alpha_beta[:], both(log_ratio[:]))
+            w = got["inv_q_den_sn"]
 
-        norms_and_codes(0, nc.scalar.copy)
-        x_scalars(0)
-        norms_and_codes(1, nc.vector.tensor_copy)
-        x_scalars(1)
-        sums(0)
-        start_scalars(0)
-        sums(1)
-        start_scalars(1)
+            def take_logs():
+                nc.scalar.activation(out=logs[:, 0, :], in_=sn[:], func=ACT.Ln, scale=1.0, bias=one[:, 0:1])
+                nc.scalar.activation(out=logs[:, 1, :], in_=sn[:], func=ACT.Ln, scale=-1.0, bias=one[:, 0:1])
+
+            def least():
+                nc.vector.tensor_scalar(out=sn[:], in0=sn[:], scalar1=MAX_NORM, scalar2=None, op0=ALU.min)
+                take_logs()
+
+            return [
+                lambda: v_mul(inv_den_sn[:], w[:], got["p_q"][:, 1, :]),
+                lambda: v_two(alpha, got["nums"][:, 1, :], 0.5, got["p_q"][:, 0, :]),
+                lambda: v_mul(sn[:], got["nums"][:, 0, :], inv_den_sn[:]),
+                lambda: v_two(beta, got["z"][:], two_hb_scale[:, 0:1], inv_den_sn[:]),
+                least,
+                lambda: v_mul(alpha, alpha, got["inv_mn"][:]),
+                lambda: v_mul(alpha, alpha, w[:]),
+                lambda: v_op(log_ratio[:], logs[:, 0, :], logs[:, 1, :], ALU.subtract),
+                lambda: v_mul(alpha_beta[:], alpha_beta[:], both(log_ratio[:])),
+            ]
 
         a_codes = keep.tile([P, GRAPHS, NODES], U32, align_bytes=64)
         a_scales = keep.tile([P, GRAPHS, NODES], U8, align_bytes=64)
+        a_grouped = {}
 
-        def quantise_adj(copy_out):
-            waiting = None
-            for b in range(GRAPHS):
-                for pair in range(TILES_PER_GRAPH // 2):
-                    cols = slice(pair * 2 * P, (pair + 1) * 2 * P)
-                    words = a_nat[:, b, 2 * pair : 2 * pair + 2, :].rearrange("p m j -> p (m j)").bitcast(F32)
-                    grouped = flip(words, nc.vector.tensor_copy if b < GRAPHS_PER_GROUP else nc.scalar.copy)
-                    if waiting is not None:
-                        quantise(*waiting)
-                    waiting = (grouped[:], a_codes[:, b, cols], a_scales[:, b, cols])
-            quantise(*waiting)
+        def flip_adj(b, pair, copy_out):
+            words = a_nat[:, b, 2 * pair : 2 * pair + 2, :].rearrange("p m j -> p (m j)").bitcast(F32)
+            a_grouped[b, pair] = flip(words, copy_out)
 
-        tangent = [{} for b in range(GRAPHS)]
+        def quantise_adj(b, pair):
+            cols = slice(pair * 2 * P, (pair + 1) * 2 * P)
+            quantise(a_grouped[b, pair][:], a_codes[:, b, cols], a_scales[:, b, cols])
 
-        def spread_bias(b):
-            tangent[b]["beta_hb"] = []
-            for t in range(TILES_PER_GRAPH):
-                grp, i = divmod(b * TILES_PER_GRAPH + t, n)
-                beta_hb = bias_pool.tile([P, FEATS], F32)
-                nc.scalar.activation(out=beta_hb[:], in_=hb[:], func=ACT.Copy, scale=scalars[grp]["alpha_beta"][:, 1, i : i + 1])
-                tangent[b]["beta_hb"].append(beta_hb)
+        UNIT_LIST = [(b, h * BANK, BANK) for b in range(GRAPHS) for h in range(HALVES)]
+        UNITS = len(UNIT_LIST)
+        tangent = [{} for j in range(UNITS)]
 
-        def tangent_tile(b, t):
+        def spread_bias(j, t):
+            b, first, width = UNIT_LIST[j]
+            grp, i = locate(b * TILES_PER_GRAPH + t)
+            beta_hb = bias_pool.tile([P, BANK], F32)
+            nc.scalar.activation(
+                out=beta_hb[:, 0:width], in_=b2_all[:, first : first + width], func=ACT.Copy,
+                scale=scalars[grp]["alpha_beta"][:, 1, i : i + 1],
+            )
+            tangent[j]["bias", t] = beta_hb
+
+        def tangent_tile(j, t):
+            b, first, width = UNIT_LIST[j]
             if t == 0:
-                tangent[b]["planes"] = tan_pool.tile([P, PACK, FEATS], BF16, name="planes")
-            grp, i = divmod(b * TILES_PER_GRAPH + t, n)
-            alpha_beta = scalars[grp]["alpha_beta"]
-            beta_hb = tangent[b]["beta_hb"][t]
-            for h in range(HALVES):
-                cols = slice(h * BANK, (h + 1) * BANK)
-                acc = project(b * TILES_PER_GRAPH + t, h)
-                nc.vector.scalar_tensor_tensor(
-                    out=tangent[b]["planes"][:, t, cols], in0=acc[:], scalar=alpha_beta[:, 0, i : i + 1], in1=beta_hb[:, cols],
-                    op0=ALU.mult, op1=ALU.add,
-                )
+                tangent[j]["planes"] = planes_pool.tile([P, PACK, BANK], BF16, name="planes")
+            grp, i = locate(b * TILES_PER_GRAPH + t)
+            acc = project(b * TILES_PER_GRAPH + t, first, width)
+            nc.vector.scalar_tensor_tensor(
+                out=tangent[j]["planes"][:, t, 0:width], in0=acc[:, 0:width],
+                scalar=scalars[grp]["alpha_beta"][:, 0, i : i + 1],
+                in1=tangent[j]["bias", t][:, 0:width], op0=ALU.mult, op1=ALU.add,
+            )
 
-        def quantise_tangent(b):
-            planes = tangent[b]["planes"]
-            t_grouped = tan_pool.tile([P, FEATS, PACK], BF16, align_bytes=64)
-            t_codes = tan_pool.tile([P, FEATS], U32, align_bytes=64)
-            t_scales = tan_pool.tile([P, FEATS], U8, align_bytes=64)
-            for h in range(HALVES):
-                cols = slice(h * BANK, (h + 1) * BANK)
-                regroup(t_grouped[:, cols, :], planes[:, :, cols])
-            for h in range(HALVES):
-                cols = slice(h * BANK, (h + 1) * BANK)
-                quantise(t_grouped[:, cols, :].rearrange("p c t -> p (c t)"), t_codes[:, cols], t_scales[:, cols])
-            tangent[b]["codes"] = t_codes
-            tangent[b]["scales"] = t_scales
+        def group_tangent(j):
+            width = UNIT_LIST[j][2]
+            tangent[j]["grouped"] = tan_pool.tile([P, BANK, PACK], BF16, align_bytes=64, name="t_grouped")
+            regroup(tangent[j]["grouped"][:, 0:width, :], tangent[j]["planes"][:, :, 0:width])
 
-        def aggregate_tile(b, m):
-            result = out_pool.tile([P, FEATS], F32)
-            for h in range(HALVES):
-                cols = slice(h * BANK, (h + 1) * BANK)
-                agg = psum.tile([P, BANK], F32, tag="bank")
-                nc.tensor.matmul_mx(
-                    out=agg[:],
-                    lhsT=a_codes[:, b, m * P : (m + 1) * P].bitcast(FP8X4),
-                    lhsT_scale=a_scales[:, b, m * P : (m + 1) * P],
-                    rhs=tangent[b]["codes"][:, cols].bitcast(FP8X4),
-                    rhs_scale=tangent[b]["scales"][:, cols],
-                    start=True,
-                    stop=True,
-                )
-                if b == GRAPHS - 1 and h == 1:
-                    nc.vector.tensor_scalar(out=result[:, cols], in0=agg[:], scalar1=0.0, scalar2=None, op0=ALU.max)
-                else:
-                    nc.scalar.activation(out=result[:, cols], in_=agg[:], func=ACT.Relu)
-            nc.sync.dma_start(out=out[b].rearrange("(p m) f -> p m f", m=TILES_PER_GRAPH)[:, m, :], in_=result[:])
+        def quantise_tangent(j):
+            width = UNIT_LIST[j][2]
+            tangent[j]["codes"] = tan_pool.tile([P, BANK], U32, align_bytes=64, name="t_codes")
+            tangent[j]["scales"] = tan_pool.tile([P, BANK], U8, align_bytes=64, name="t_scales")
+            quantise(
+                tangent[j]["grouped"][:, 0:width, :].rearrange("p c t -> p (c t)"),
+                tangent[j]["codes"][:, 0:width], tangent[j]["scales"][:, 0:width],
+            )
 
-        quantise_adj(nc.scalar.copy)
-        take_logs(0)
-        finish_scalars(0)
-        spread_bias(0)
+        def aggregate_tile(j, m):
+            b, first, width = UNIT_LIST[j]
+            if m % 2 == 0:
+                tangent[j]["result"] = out_pool.tile([P, 2, BANK], F32, name="result")
+            result = tangent[j]["result"]
+            agg = psum.tile([P, BANK], F32, tag="bank")
+            nc.tensor.matmul_mx(
+                out=agg[:, 0:width],
+                lhsT=a_codes[:, b, m * P : (m + 1) * P].bitcast(FP8X4),
+                lhsT_scale=a_scales[:, b, m * P : (m + 1) * P],
+                rhs=tangent[j]["codes"][:, 0:width].bitcast(FP8X4),
+                rhs_scale=tangent[j]["scales"][:, 0:width],
+                start=True,
+                stop=True,
+            )
+            if (j == UNITS - 1 and m % 2 == 1) or (j, m) in VRELU:
+                nc.vector.tensor_scalar(out=result[:, m % 2, 0:width], in0=agg[:, 0:width], scalar1=0.0, scalar2=None, op0=ALU.max)
+            else:
+                nc.scalar.activation(out=result[:, m % 2, 0:width], in_=agg[:, 0:width], func=ACT.Relu)
+            view = out[b].rearrange("(p m) f -> p m f", m=TILES_PER_GRAPH)[:, :, first : first + width]
+            if j == UNITS - 1:
+                nc.sync.dma_start(out=view[:, m, :], in_=result[:, m % 2, 0:width])
+            elif m % 2 == 1:
+                nc.sync.dma_start(out=view[:, m - 1 : m + 1, :], in_=result[:, :, 0:width])
+
+        bias_scalars()
+        square_x(0)
+        flip_x(0, nc.scalar.copy)
+        square_x(1)
+        flip_x(1, nc.scalar.copy)
+        group_w(0, 0)
+        group_w(0, 1)
+        quantise_w(0, 0)
+        quantise_w(0, 1)
+        quantise_x(0)
+
+        grams = {}
+
+        def prepare(col):
+            if col < ROW_TILES:
+                if col not in GRAM:
+                    square_x(col)
+                flip_x(col, nc.scalar.copy if col in FS else nc.vector.tensor_copy)
+            if 1 <= col - 1 < ROW_TILES:
+                quantise_x(col - 1)
+            if 1 <= col - 2 < ROW_TILES:
+                if col - 2 in GRAM:
+                    grams[col - 2] = gram_x(col - 2)
+            if col - 3 in grams:
+                diagonal(col - 3, grams[col - 3])
+
+        LEAD = 19
+        VRELU = ()
+        FS = (2,3,4,6,8,10,12,14)
+        GRAM = (5, 7, 9, 11, 13)
+        for col in range(2, LEAD):
+            prepare(col)
+            if col == 10:
+                x_scalars(0)
+            if col == 3:
+                group_w(1, 0)
+            if col == 4:
+                group_w(1, 1)
+                quantise_w(1, 0)
+            if col == 5:
+                quantise_w(1, 1)
+        x_scalars(1)
+
+        for col in range(ROW_TILES):
+            acc = [project(col, h * BANK, BANK) for h in range(HALVES)]
+            for h in range(HALVES):
+                dot_hb(col, h, acc[h])
+                square_mx(col, h, acc[h])
+            if col == 7:
+                norm_mx(0)
+                start_scalars(0)
+                root_scalars(0)
+            if col in (14, 15):
+                flip_adj(0, col - 14, nc.scalar.copy)
+        norm_mx(1)
+        start_scalars(1)
+        root_scalars(1)
+        flips = [(b, pair) for b in range(1, GRAPHS) for pair in range(2)]
+        for k in range(3):
+            flip_adj(*flips[k], nc.vector.tensor_copy)
+        for op in late_ops(0):
+            op()
+        quantise_adj(0, 0)
+        quantise_adj(0, 1)
         for t in range(TILES_PER_GRAPH):
-            tangent_tile(0, t)
-        quantise_tangent(0)
-        spread_bias(1)
-        for b in range(GRAPHS):
-            if b + 1 < GRAPHS:
-                tangent_tile(b + 1, 0)
+            spread_bias(0, t)
+        for t in range(TILES_PER_GRAPH):
+            spread_bias(1, t)
+        for j in range(UNITS + 1):
+            b = UNIT_LIST[j][0] if j < UNITS else GRAPHS
+            fresh = 0 < j < UNITS and UNIT_LIST[j - 1][0] != b
             for t in range(TILES_PER_GRAPH):
-                if b + 1 < GRAPHS and t + 1 < TILES_PER_GRAPH:
-                    tangent_tile(b + 1, t + 1)
-                if b + 2 == GRAPHS_PER_GROUP and t == TILES_PER_GRAPH - 1:
-                    take_logs(1)
-                aggregate_tile(b, t)
-            if b + 2 < GRAPHS and (b + 2) % GRAPHS_PER_GROUP == 0:
-                finish_scalars((b + 2) // GRAPHS_PER_GROUP)
-            if b + 1 < GRAPHS:
-                quantise_tangent(b + 1)
-            if b + 2 < GRAPHS:
-                spread_bias(b + 2)
+                if j < UNITS:
+                    tangent_tile(j, t)
+                if j > 0 and t == 0:
+                    group_tangent(j - 1)
+                if j > 0 and t == 2:
+                    quantise_tangent(j - 1)
+                if fresh and t in (1, 3):
+                    quantise_adj(b, t // 2)
+                if j >= 2:
+                    aggregate_tile(j - 2, t)
+                if j == 0:
+                    spread_bias(2, t)
+                if j == 1:
+                    spread_bias(3, t)
+                if j == 2 and t == 2:
+                    ops = late_ops(1)
+                if j == 2 and t == 3:
+                    for op in ops[0:5]:
+                        op()
+                if j == 3 and t == 0:
+                    for op in ops[5:9]:
+                        op()
+                if j == 3 and t >= 2:
+                    spread_bias(4, 2 * t - 4)
+                    spread_bias(4, 2 * t - 3)
+                if 4 <= j and j + 1 < UNITS:
+                    spread_bias(j + 1, t)
+                if j in (1, 3) and t in (1, 3):
+                    k = 3 + (j - 1) + t // 2
+                    if k < 6:
+                        flip_adj(*flips[k], nc.scalar.copy)
+        for t in range(TILES_PER_GRAPH):
+            aggregate_tile(UNITS - 1, t)

@@ -94,7 +94,7 @@ def tile_module_1_pb_kernel(tc, adj, x1, W2, b2, out):
         make_identity(nc, ident[:])
         neg_half = const.tile([P, ROW_TILES], F32)
         nc.gpsimd.memset(neg_half[:], -0.5)
-        neg_one = const.tile([P, ROW_TILES], F32)
+        neg_one = const.tile([P, 1], F32)
         nc.gpsimd.memset(neg_one[:], -1.0)
         warm = const.tile([P, 1], F32)
         nc.scalar.activation(out=warm[:], in_=one_half[:], func=ACT.Ln)
@@ -252,17 +252,17 @@ def tile_module_1_pb_kernel(tc, adj, x1, W2, b2, out):
         def v_op(o, a, b, op):
             nc.vector.tensor_tensor(out=o, in0=a, in1=b, op=op)
 
-        def x_scalars(grp):
-            n = GROUP_TILES[grp]
-            mine = slice(GROUP_FIRST[grp], GROUP_FIRST[grp] + n)
-            g_one(xn[:, mine], xn[:, mine], TINY, ALU.max)
-            g_pow(inv_xn[:, mine], xn[:, mine], neg_half[:, 0:n])
-            g_mul(xn[:, mine], xn[:, mine], inv_xn[:, mine])
-            g_one(zb[:, mine], xn[:, mine], ARTANH_CLIP, ALU.min)
-            g_affine(one_plus[:, mine], zb[:, mine], 1.0, 1.0)
-            g_affine(zb[:, mine], zb[:, mine], -1.0, 1.0)
-            g_pow(one_plus[:, mine], one_plus[:, mine], neg_one[:, 0:n])
-            g_mul(zb[:, mine], zb[:, mine], one_plus[:, mine])
+        def x_scalars():
+            g_one(xn[:], xn[:], TINY, ALU.max)
+            g_pow(inv_xn[:], xn[:], neg_half[:])
+            g_mul(xn[:], xn[:], inv_xn[:])
+            g_one(zb[:], xn[:], ARTANH_CLIP, ALU.min)
+            g_affine(one_plus[:], zb[:], 1.0, 1.0)
+            g_affine(zb[:], zb[:], -1.0, 1.0)
+
+        def x_ratio():
+            nc.vector.reciprocal(out=one_plus[:], in_=one_plus[:])
+            g_mul(zb[:], zb[:], one_plus[:])
 
         for grp in range(GROUPS):
             scalars[grp]["parts"] = small.tile([P, HALVES, 2, GROUP_TILES[grp]], F32, name="parts%d" % grp)
@@ -289,7 +289,8 @@ def tile_module_1_pb_kernel(tc, adj, x1, W2, b2, out):
         def norm_mx(grp):
             parts = scalars[grp]["parts"]
             mn_e2 = double(grp, "mn_e2")
-            g_op(mn_e2[:], parts[:, 0], parts[:, 1], ALU.add)
+            add = nc.gpsimd.tensor_tensor if grp == 0 else nc.vector.tensor_tensor
+            add(out=mn_e2[:], in0=parts[:, 0], in1=parts[:, 1], op=ALU.add)
 
         def start_scalars(grp):
             got = scalars[grp]
@@ -404,7 +405,12 @@ def tile_module_1_pb_kernel(tc, adj, x1, W2, b2, out):
         def group_tangent(j):
             width = UNIT_LIST[j][2]
             tangent[j]["grouped"] = tan_pool.tile([P, BANK, PACK], BF16, align_bytes=64, name="t_grouped")
-            regroup(tangent[j]["grouped"][:, 0:width, :], tangent[j]["planes"][:, :, 0:width])
+            dst, src = tangent[j]["grouped"][:, 0:width, :], tangent[j]["planes"][:, :, 0:width]
+            copy = nc.scalar.copy if j in SRG else nc.vector.tensor_copy
+            copy(
+                out=dst.rearrange("p (c i) t -> p c t i", i=4),
+                in_=src.rearrange("p t (c i) -> p c t i", i=4),
+            )
 
         def quantise_tangent(j):
             width = UNIT_LIST[j][2]
@@ -466,14 +472,12 @@ def tile_module_1_pb_kernel(tc, adj, x1, W2, b2, out):
             if col - 3 in grams:
                 diagonal(col - 3, grams[col - 3])
 
-        LEAD = 19
+        LEAD = 17
         VRELU = ()
-        FS = (2,3,4,6,8,10,12,14)
-        GRAM = (5, 7, 9, 11, 13)
+        FS = (2,3)
+        GRAM = ()
         for col in range(2, LEAD):
             prepare(col)
-            if col == 10:
-                x_scalars(0)
             if col == 3:
                 group_w(1, 0)
             if col == 4:
@@ -481,57 +485,66 @@ def tile_module_1_pb_kernel(tc, adj, x1, W2, b2, out):
                 quantise_w(1, 0)
             if col == 5:
                 quantise_w(1, 1)
-        x_scalars(1)
 
         for col in range(ROW_TILES):
             acc = [project(col, h * BANK, BANK) for h in range(HALVES)]
             for h in range(HALVES):
                 dot_hb(col, h, acc[h])
                 square_mx(col, h, acc[h])
+            if LEAD + col < ROW_TILES + 3:
+                prepare(LEAD + col)
+            if col == 0:
+                x_scalars()
+            if col == 5:
+                x_ratio()
             if col == 7:
                 norm_mx(0)
                 start_scalars(0)
                 root_scalars(0)
-            if col in (14, 15):
-                flip_adj(0, col - 14, nc.scalar.copy)
+        VF = ((0,0),(2,1))
+        SRG = ()
+        for b in (0, 2, 1, 3):
+            for pair in range(2):
+                flip_adj(b, pair, nc.vector.tensor_copy if (b, pair) in VF else nc.scalar.copy)
+        quantise_adj(0, 0)
+        quantise_adj(0, 1)
+        quantise_adj(2, 0)
+        ops = late_ops(0)
+        for op in ops[0:5]:
+            op()
+        quantise_adj(2, 1)
+        quantise_adj(1, 0)
+        for op in ops[5:9]:
+            op()
         norm_mx(1)
         start_scalars(1)
         root_scalars(1)
-        flips = [(b, pair) for b in range(1, GRAPHS) for pair in range(2)]
-        for k in range(3):
-            flip_adj(*flips[k], nc.vector.tensor_copy)
-        for op in late_ops(0):
-            op()
-        quantise_adj(0, 0)
-        quantise_adj(0, 1)
+        quantise_adj(1, 1)
         for t in range(TILES_PER_GRAPH):
             spread_bias(0, t)
         for t in range(TILES_PER_GRAPH):
             spread_bias(1, t)
         for j in range(UNITS + 1):
-            b = UNIT_LIST[j][0] if j < UNITS else GRAPHS
-            fresh = 0 < j < UNITS and UNIT_LIST[j - 1][0] != b
             for t in range(TILES_PER_GRAPH):
                 if j < UNITS:
                     tangent_tile(j, t)
+                if j == 0 and t < 2:
+                    quantise_adj(3, t)
                 if j > 0 and t == 0:
                     group_tangent(j - 1)
                 if j > 0 and t == 2:
                     quantise_tangent(j - 1)
-                if fresh and t in (1, 3):
-                    quantise_adj(b, t // 2)
                 if j >= 2:
                     aggregate_tile(j - 2, t)
                 if j == 0:
                     spread_bias(2, t)
                 if j == 1:
                     spread_bias(3, t)
-                if j == 2 and t == 2:
+                if j == 3 and t == 0:
                     ops = late_ops(1)
-                if j == 2 and t == 3:
                     for op in ops[0:5]:
                         op()
-                if j == 3 and t == 0:
+                if j == 3 and t == 1:
                     for op in ops[5:9]:
                         op()
                 if j == 3 and t >= 2:
@@ -539,9 +552,5 @@ def tile_module_1_pb_kernel(tc, adj, x1, W2, b2, out):
                     spread_bias(4, 2 * t - 3)
                 if 4 <= j and j + 1 < UNITS:
                     spread_bias(j + 1, t)
-                if j in (1, 3) and t in (1, 3):
-                    k = 3 + (j - 1) + t // 2
-                    if k < 6:
-                        flip_adj(*flips[k], nc.scalar.copy)
         for t in range(TILES_PER_GRAPH):
             aggregate_tile(UNITS - 1, t)

@@ -53,6 +53,13 @@ def tile_module_1_pb_kernel(tc, adj, x1, W2, b2, out):
         w_raw = keep.tile([P, K_PASSES, PACK, FEATS], BF16)
         a_nat = keep.tile([P, GRAPHS, TILES_PER_GRAPH, NODES], BF16)
 
+        def load_x_tile(col):
+            b, t = divmod(col, TILES_PER_GRAPH)
+            u, e = divmod(t, 2)
+            nc.sync.dma_start(
+                out=x_nat[:, col, :], in_=x1[b][2 * P * u : 2 * P * (u + 1), :].rearrange("(p e) k -> p e k", e=2)[:, e, :]
+            )
+
         def load_x(b, u):
             first = b * TILES_PER_GRAPH + 2 * u
             nc.sync.dma_start(
@@ -68,14 +75,16 @@ def tile_module_1_pb_kernel(tc, adj, x1, W2, b2, out):
             )
 
         b2_row = const.tile([P, FEATS], BF16)
-        nc.vector.memset(b2_row[:, 0:BANK], 0.0)
-        nc.gpsimd.memset(b2_row[:, BANK:FEATS], 0.0)
-        load_x(0, 0)
-        nc.sync.dma_start(out=b2_row[0:1, :], in_=b2.rearrange("(o h) -> o h", o=1))
+        nc.vector.memset(b2_row[:], 0.0)
+        load_x_tile(0)
         load_w(0)
+        load_x_tile(1)
         load_x(0, 1)
         load_w(1)
-        for b in range(1, GRAPHS):
+        load_x(1, 0)
+        nc.sync.dma_start(out=b2_row[0:1, :], in_=b2.rearrange("(o h) -> o h", o=1))
+        load_x(1, 1)
+        for b in range(2, GRAPHS):
             load_x(b, 0)
             load_x(b, 1)
         for b in range(GRAPHS):
@@ -116,13 +125,16 @@ def tile_module_1_pb_kernel(tc, adj, x1, W2, b2, out):
 
         b2_all = const.tile([P, FEATS], F32)
         bn_parts = small.tile([P, HALVES], F32)
-        for h in range(HALVES):
-            b2_bank = psum.tile([P, BANK], F32, tag="bank")
-            cols = slice(h * BANK, (h + 1) * BANK)
-            nc.tensor.matmul(out=b2_bank[:], lhsT=ones[:], rhs=b2_row[:, cols], start=True, stop=True)
-            sq_b = unread.tile([P, BANK], BF16, name="sq_s")
-            nc.scalar.activation(out=sq_b[:], in_=b2_bank[:], func=ACT.Square, accum_out=bn_parts[:, h : h + 1])
-            nc.vector.tensor_copy(out=b2_all[:, cols], in_=b2_bank[:])
+
+        def spread_b2():
+            for h in range(HALVES):
+                b2_bank = psum.tile([P, BANK], F32, tag="bank")
+                cols = slice(h * BANK, (h + 1) * BANK)
+                nc.tensor.matmul(out=b2_bank[:], lhsT=ones[:], rhs=b2_row[:, cols], start=True, stop=True)
+                sq_b = unread.tile([P, BANK], BF16, name="sq_s")
+                nc.scalar.activation(out=sq_b[:], in_=b2_bank[:], func=ACT.Square, accum_out=bn_parts[:, h : h + 1])
+                nc.vector.tensor_copy(out=b2_all[:, cols], in_=b2_bank[:])
+
         bn = small.tile([P, 1], F32)
         inv_bn = small.tile([P, 1], F32)
         decay = small.tile([P, 1], F32)
@@ -364,6 +376,11 @@ def tile_module_1_pb_kernel(tc, adj, x1, W2, b2, out):
                 lambda: v_mul(alpha_beta[:], alpha_beta[:], both(log_ratio[:])),
             ]
 
+        def residual(grp):
+            norm_mx(grp)
+            start_scalars(grp)
+            root_scalars(grp)
+
         a_codes = keep.tile([P, GRAPHS, NODES], U32, align_bytes=64)
         a_scales = keep.tile([P, GRAPHS, NODES], U8, align_bytes=64)
         a_grouped = {}
@@ -446,7 +463,6 @@ def tile_module_1_pb_kernel(tc, adj, x1, W2, b2, out):
             elif m % 2 == 1:
                 nc.sync.dma_start(out=view[:, m - 1 : m + 1, :], in_=result[:, :, 0:width])
 
-        bias_scalars()
         square_x(0)
         flip_x(0, nc.scalar.copy)
         square_x(1)
@@ -478,6 +494,9 @@ def tile_module_1_pb_kernel(tc, adj, x1, W2, b2, out):
         GRAM = ()
         for col in range(2, LEAD):
             prepare(col)
+            if col == 6:
+                spread_b2()
+                bias_scalars()
             if col == 3:
                 group_w(1, 0)
             if col == 4:
@@ -495,61 +514,68 @@ def tile_module_1_pb_kernel(tc, adj, x1, W2, b2, out):
                 prepare(LEAD + col)
             if col == 0:
                 x_scalars()
-            if col == 5:
+            if col == 4:
                 x_ratio()
             if col == 7:
-                norm_mx(0)
-                start_scalars(0)
-                root_scalars(0)
-        VF = ((0,0),(2,1))
+                residual(0)
         SRG = ()
+        VF = ()
         for b in (0, 2, 1, 3):
             for pair in range(2):
                 flip_adj(b, pair, nc.vector.tensor_copy if (b, pair) in VF else nc.scalar.copy)
+        ops = late_ops(0)
         quantise_adj(0, 0)
         quantise_adj(0, 1)
+        ops[0]()
         quantise_adj(2, 0)
-        ops = late_ops(0)
-        for op in ops[0:5]:
-            op()
+        ops[2]()
+        ops[1]()
         quantise_adj(2, 1)
+        ops[4]()
         quantise_adj(1, 0)
-        for op in ops[5:9]:
-            op()
-        norm_mx(1)
-        start_scalars(1)
-        root_scalars(1)
+        ops[3]()
+        ops[5]()
+        ops[7]()
         quantise_adj(1, 1)
+        ops[6]()
+        quantise_adj(3, 0)
+        ops[8]()
+        residual(1)
         for t in range(TILES_PER_GRAPH):
             spread_bias(0, t)
         for t in range(TILES_PER_GRAPH):
             spread_bias(1, t)
+        late = {}
         for j in range(UNITS + 1):
             for t in range(TILES_PER_GRAPH):
                 if j < UNITS:
                     tangent_tile(j, t)
-                if j == 0 and t < 2:
-                    quantise_adj(3, t)
+                if j == 0 and t == 0:
+                    quantise_adj(3, 1)
+                if j == 2 and t == 3:
+                    late[1] = late_ops(1)
+                if j == 3:
+                    k = (0, 2, 5, 7)[t]
+                    order = (0, 2, 4, 1, 3, 5, 7, 6, 8)
+                    late[1][order[k]]()
                 if j > 0 and t == 0:
                     group_tangent(j - 1)
+                if j == 3:
+                    late[1][order[k + 1]]()
                 if j > 0 and t == 2:
                     quantise_tangent(j - 1)
+                if j == 3 and t == 1:
+                    if t == 1:
+                        late[1][order[4]]()
                 if j >= 2:
                     aggregate_tile(j - 2, t)
                 if j == 0:
                     spread_bias(2, t)
                 if j == 1:
                     spread_bias(3, t)
-                if j == 3 and t == 0:
-                    ops = late_ops(1)
-                    for op in ops[0:5]:
-                        op()
-                if j == 3 and t == 1:
-                    for op in ops[5:9]:
-                        op()
-                if j == 3 and t >= 2:
-                    spread_bias(4, 2 * t - 4)
-                    spread_bias(4, 2 * t - 3)
+                if j == 3 and t == 3:
+                    for k in range(TILES_PER_GRAPH):
+                        spread_bias(4, k)
                 if 4 <= j and j + 1 < UNITS:
                     spread_bias(j + 1, t)
         for t in range(TILES_PER_GRAPH):

@@ -42,9 +42,9 @@ def tile_module_1_pb_kernel(tc, adj, x1, W2, b2, out):
         stage = ctx.enter_context(tc.tile_pool(name="stage", bufs=2))
         unread = ctx.enter_context(tc.tile_pool(name="unread", bufs=2))
         tan_pool = ctx.enter_context(tc.tile_pool(name="tan", bufs=3))
-        planes_pool = ctx.enter_context(tc.tile_pool(name="planes", bufs=5))
-        bias_pool = ctx.enter_context(tc.tile_pool(name="bias", bufs=16))
-        out_pool = ctx.enter_context(tc.tile_pool(name="outs", bufs=4))
+        planes_pool = ctx.enter_context(tc.tile_pool(name="planes", bufs=3))
+        bias_pool = ctx.enter_context(tc.tile_pool(name="bias", bufs=12))
+        out_pool = ctx.enter_context(tc.tile_pool(name="outs", bufs=6))
         rows_pool = ctx.enter_context(tc.tile_pool(name="rows", bufs=8))
         psum = ctx.enter_context(tc.psum_pool(name="psum", bufs=8))
         ctx.enter_context(tc.manual_schedule())
@@ -488,10 +488,10 @@ def tile_module_1_pb_kernel(tc, adj, x1, W2, b2, out):
             if col - 3 in grams:
                 diagonal(col - 3, grams[col - 3])
 
-        LEAD = 17
+        LEAD = 19
         VRELU = ()
-        FS = (2,3)
-        GRAM = ()
+        FS = (2,3,5,7,9,11,13,15)
+        GRAM = (5,7,9,11,13)
         for col in range(2, LEAD):
             prepare(col)
             if col == 6:

@@ -43,8 +43,8 @@ def tile_module_1_pb_kernel(tc, adj, x1, W2, b2, out):
         unread = ctx.enter_context(tc.tile_pool(name="unread", bufs=2))
         tan_pool = ctx.enter_context(tc.tile_pool(name="tan", bufs=3))
         planes_pool = ctx.enter_context(tc.tile_pool(name="planes", bufs=3))
-        bias_pool = ctx.enter_context(tc.tile_pool(name="bias", bufs=12))
-        out_pool = ctx.enter_context(tc.tile_pool(name="outs", bufs=6))
+        bias_pool = ctx.enter_context(tc.tile_pool(name="bias", bufs=16))
+        out_pool = ctx.enter_context(tc.tile_pool(name="outs", bufs=5))
         rows_pool = ctx.enter_context(tc.tile_pool(name="rows", bufs=8))
         psum = ctx.enter_context(tc.psum_pool(name="psum", bufs=8))
         ctx.enter_context(tc.manual_schedule())
@@ -101,12 +101,14 @@ def tile_module_1_pb_kernel(tc, adj, x1, W2, b2, out):
         nc.gpsimd.memset(one_half[:], 0.5)
         ident = const.tile([P, P], F32)
         make_identity(nc, ident[:])
+        tiny = const.tile([P, 1], F32)
+        nc.gpsimd.memset(tiny[:], TINY)
         neg_half = const.tile([P, ROW_TILES], F32)
         nc.gpsimd.memset(neg_half[:], -0.5)
         neg_one = const.tile([P, 1], F32)
         nc.gpsimd.memset(neg_one[:], -1.0)
         warm = const.tile([P, 1], F32)
-        nc.scalar.activation(out=warm[:], in_=one_half[:], func=ACT.Ln)
+        nc.scalar.activation(out=warm[:], in_=one_half[:], func=ACT.Sqrt)
 
         def g_op(o, a, b, op):
             nc.gpsimd.tensor_tensor(out=o, in0=a, in1=b, op=op)
@@ -265,14 +267,13 @@ def tile_module_1_pb_kernel(tc, adj, x1, W2, b2, out):
             nc.vector.tensor_tensor(out=o, in0=a, in1=b, op=op)
 
         def x_scalars():
-            g_one(xn[:], xn[:], TINY, ALU.max)
-            g_pow(inv_xn[:], xn[:], neg_half[:])
-            g_mul(xn[:], xn[:], inv_xn[:])
+            nc.scalar.activation(out=xn[:], in_=xn[:], func=ACT.Sqrt, scale=1.0, bias=tiny[:, 0:1])
             g_one(zb[:], xn[:], ARTANH_CLIP, ALU.min)
             g_affine(one_plus[:], zb[:], 1.0, 1.0)
             g_affine(zb[:], zb[:], -1.0, 1.0)
 
         def x_ratio():
+            nc.vector.reciprocal(out=inv_xn[:], in_=xn[:])
             nc.vector.reciprocal(out=one_plus[:], in_=one_plus[:])
             g_mul(zb[:], zb[:], one_plus[:])
 
@@ -298,11 +299,15 @@ def tile_module_1_pb_kernel(tc, adj, x1, W2, b2, out):
         def v_two(o, a, scalar, b):
             nc.vector.scalar_tensor_tensor(out=o, in0=a, scalar=scalar, in1=b, op0=ALU.mult, op1=ALU.mult)
 
-        def norm_mx(grp):
+        def sum_mx(grp):
             parts = scalars[grp]["parts"]
             mn_e2 = double(grp, "mn_e2")
-            add = nc.gpsimd.tensor_tensor if grp == 0 else nc.vector.tensor_tensor
-            add(out=mn_e2[:], in0=parts[:, 0], in1=parts[:, 1], op=ALU.add)
+            g_op(mn_e2[:], parts[:, 0], parts[:, 1], ALU.add)
+
+        def root_mx(grp):
+            mn_e2 = scalars[grp]["mn_e2"]
+            if grp == 0:
+                nc.scalar.activation(out=mn_e2[:, 0, :], in_=mn_e2[:, 0, :], func=ACT.Sqrt, scale=1.0, bias=tiny[:, 0:1])
 
         def start_scalars(grp):
             got = scalars[grp]
@@ -310,9 +315,12 @@ def tile_module_1_pb_kernel(tc, adj, x1, W2, b2, out):
             mine = slice(GROUP_FIRST[grp], GROUP_FIRST[grp] + n)
             mn, e2 = got["mn_e2"][:, 0, :], got["mn_e2"][:, 1, :]
             inv_mn = single(grp, "inv_mn")
-            g_one(mn, mn, TINY, ALU.max)
-            g_pow(inv_mn[:], mn, neg_half[:, 0:n])
-            g_mul(mn, mn, inv_mn[:])
+            if grp == 0:
+                nc.vector.reciprocal(out=inv_mn[:], in_=mn)
+            else:
+                g_one(mn, mn, TINY, ALU.max)
+                g_pow(inv_mn[:], mn, neg_half[:, 0:n])
+                g_mul(mn, mn, inv_mn[:])
             z = single(grp, "z")
             g_mul(z[:], mn, inv_xn[:, mine])
             g_pow(z[:], zb[:, mine], z[:])
@@ -377,7 +385,7 @@ def tile_module_1_pb_kernel(tc, adj, x1, W2, b2, out):
             ]
 
         def residual(grp):
-            norm_mx(grp)
+            sum_mx(grp)
             start_scalars(grp)
             root_scalars(grp)
 
@@ -453,7 +461,7 @@ def tile_module_1_pb_kernel(tc, adj, x1, W2, b2, out):
                 start=True,
                 stop=True,
             )
-            if (j == UNITS - 1 and m % 2 == 1) or (j, m) in VRELU:
+            if (j == UNITS - 1 and m % 2 == 1):
                 nc.vector.tensor_scalar(out=result[:, m % 2, 0:width], in0=agg[:, 0:width], scalar1=0.0, scalar2=None, op0=ALU.max)
             else:
                 nc.scalar.activation(out=result[:, m % 2, 0:width], in_=agg[:, 0:width], func=ACT.Relu)
@@ -514,65 +522,59 @@ def tile_module_1_pb_kernel(tc, adj, x1, W2, b2, out):
                 prepare(LEAD + col)
             if col == 0:
                 x_scalars()
-            if col == 4:
+            if col == 2:
                 x_ratio()
             if col == 7:
-                residual(0)
-        SRG = ()
-        VF = ()
-        for b in (0, 2, 1, 3):
-            for pair in range(2):
-                flip_adj(b, pair, nc.vector.tensor_copy if (b, pair) in VF else nc.scalar.copy)
-        ops = late_ops(0)
-        quantise_adj(0, 0)
-        quantise_adj(0, 1)
-        ops[0]()
-        quantise_adj(2, 0)
-        ops[2]()
-        ops[1]()
-        quantise_adj(2, 1)
-        ops[4]()
-        quantise_adj(1, 0)
-        ops[3]()
-        ops[5]()
-        ops[7]()
-        quantise_adj(1, 1)
-        ops[6]()
-        quantise_adj(3, 0)
-        ops[8]()
+                sum_mx(0)
+            if col == 8:
+                root_mx(0)
+                start_scalars(0)
+                root_scalars(0)
+            if col == 10:
+                nc.scalar.activation(out=warm[:], in_=one_half[:], func=ACT.Ln)
+            if col == 14:
+                ops = late_ops(0)
+            if 14 <= col:
+                for k in ((0, 2, 1, 4, 3), (5, 7, 6, 8))[col - 14]:
+                    ops[k]()
         residual(1)
+        SRG = (2,)
+        SC, VC = nc.scalar.copy, nc.vector.tensor_copy
+        FLIPS = {(0, 1): (2, 0, VC), (0, 3): (2, 1, VC), (1, 1): (1, 0, SC), (1, 3): (1, 1, SC), (2, 1): (3, 0, SC), (2, 3): (3, 1, SC)}
         for t in range(TILES_PER_GRAPH):
             spread_bias(0, t)
+        for pair in range(2):
+            flip_adj(0, pair, nc.scalar.copy)
         for t in range(TILES_PER_GRAPH):
             spread_bias(1, t)
-        late = {}
+        order = (0, 2, 1, 4, 3, 5, 7, 6, 8)
         for j in range(UNITS + 1):
+            b, h = divmod(j, HALVES)
             for t in range(TILES_PER_GRAPH):
                 if j < UNITS:
                     tangent_tile(j, t)
-                if j == 0 and t == 0:
-                    quantise_adj(3, 1)
-                if j == 2 and t == 3:
-                    late[1] = late_ops(1)
-                if j == 3:
-                    k = (0, 2, 5, 7)[t]
-                    order = (0, 2, 4, 1, 3, 5, 7, 6, 8)
-                    late[1][order[k]]()
+                if (j, t) in FLIPS:
+                    flip_adj(FLIPS[j, t][0], FLIPS[j, t][1], FLIPS[j, t][2])
                 if j > 0 and t == 0:
                     group_tangent(j - 1)
-                if j == 3:
-                    late[1][order[k + 1]]()
+                if j == 0 and t == 3:
+                    quantise_adj(0, 0)
+                    quantise_adj(0, 1)
                 if j > 0 and t == 2:
                     quantise_tangent(j - 1)
-                if j == 3 and t == 1:
-                    if t == 1:
-                        late[1][order[4]]()
+                if j > 2 and j < UNITS and h == 1 and t in (1, 3):
+                    quantise_adj(b + 0, t // 2)
                 if j >= 2:
                     aggregate_tile(j - 2, t)
                 if j == 0:
                     spread_bias(2, t)
                 if j == 1:
                     spread_bias(3, t)
+                if j == 3:
+                    if t == 0:
+                        late = late_ops(1)
+                    for k in (order[0:2], order[2:4], order[4:6], order[6:9])[t]:
+                        late[k]()
                 if j == 3 and t == 3:
                     for k in range(TILES_PER_GRAPH):
                         spread_bias(4, k)

import math
from contextlib import ExitStack

import concourse.mybir as mybir
from concourse.masks import make_identity

F32 = mybir.dt.float32
BF16 = mybir.dt.bfloat16
U32 = mybir.dt.uint32
U8 = mybir.dt.uint8
FP8X4 = mybir.dt.float8_e4m3fn_x4
ALU = mybir.AluOpType
ACT = mybir.ActivationFunctionType

P = 128
PACK = 4
BANK = 512
GRAPHS, NODES, FEATS = 4, 512, 1024
TILES_PER_GRAPH = NODES // P
ROW_TILES = GRAPHS * TILES_PER_GRAPH
K_PASSES = FEATS // (P * PACK)
HALVES = FEATS // BANK
GROUP_TILES = (8, 8)
GROUP_FIRST = (0, 8)
GROUPS = len(GROUP_TILES)
GROUP_OF = [grp for grp in range(GROUPS) for i in range(GROUP_TILES[grp])]

MIN_NORM_SQ = 1e-30
MAX_NORM = 0.996
ARTANH_CLIP = 1.0 - 1e-7
TINY = 2.0**-100

FLOPS = 2 * GRAPHS * NODES * FEATS * FEATS + 2 * GRAPHS * NODES * NODES * FEATS


def tile_module_1_pb_kernel(tc, adj, x1, W2, b2, out):
    nc = tc.nc
    with ExitStack() as ctx:
        const = ctx.enter_context(tc.tile_pool(name="const", bufs=1))
        keep = ctx.enter_context(tc.tile_pool(name="keep", bufs=1))
        small = ctx.enter_context(tc.tile_pool(name="small", bufs=1))
        stage = ctx.enter_context(tc.tile_pool(name="stage", bufs=2))
        unread = ctx.enter_context(tc.tile_pool(name="unread", bufs=2))
        tan_pool = ctx.enter_context(tc.tile_pool(name="tan", bufs=3))
        planes_pool = ctx.enter_context(tc.tile_pool(name="planes", bufs=3))
        bias_pool = ctx.enter_context(tc.tile_pool(name="bias", bufs=16))
        out_pool = ctx.enter_context(tc.tile_pool(name="outs", bufs=5))
        rows_pool = ctx.enter_context(tc.tile_pool(name="rows", bufs=8))
        psum = ctx.enter_context(tc.psum_pool(name="psum", bufs=8))
        ctx.enter_context(tc.manual_schedule())

        x_nat = keep.tile([P, ROW_TILES, FEATS], BF16)
        w_raw = keep.tile([P, K_PASSES, PACK, FEATS], BF16)
        a_nat = keep.tile([P, GRAPHS, TILES_PER_GRAPH, NODES], BF16)

        def load_x_tile(col):
            b, t = divmod(col, TILES_PER_GRAPH)
            u, e = divmod(t, 2)
            nc.sync.dma_start(
                out=x_nat[:, col, :], in_=x1[b][2 * P * u : 2 * P * (u + 1), :].rearrange("(p e) k -> p e k", e=2)[:, e, :]
            )

        def load_x(b, u):
            first = b * TILES_PER_GRAPH + 2 * u
            nc.sync.dma_start(
                out=x_nat[:, first : first + 2, :].rearrange("p e k -> p (e k)"),
                in_=x1[b][2 * P * u : 2 * P * (u + 1), :].rearrange("(p e) k -> p (e k)", e=2),
            )

        def load_w(g):
            rows = slice(g * P * PACK, (g + 1) * P * PACK)
            nc.sync.dma_start(
                out=w_raw[:, g, :, :].rearrange("p (u e) n -> p u (e n)", e=2),
                in_=W2[rows, :].rearrange("(u p e) n -> p u (e n)", u=2, e=2),
            )

        b2_row = const.tile([P, FEATS], BF16)
        nc.vector.memset(b2_row[:], 0.0)
        load_x_tile(0)
        load_w(0)
        load_x_tile(1)
        load_x(0, 1)
        load_w(1)
        load_x(1, 0)
        nc.sync.dma_start(out=b2_row[0:1, :], in_=b2.rearrange("(o h) -> o h", o=1))
        load_x(1, 1)
        for b in range(2, GRAPHS):
            load_x(b, 0)
            load_x(b, 1)
        for b in range(GRAPHS):
            nc.sync.dma_start(
                out=a_nat[:, b, :, :].rearrange("p m j -> p (m j)"),
                in_=adj[b].rearrange("(p m) j -> p (m j)", m=TILES_PER_GRAPH),
            )

        ones = const.tile([P, P], BF16)
        nc.vector.memset(ones[:], 1.0)
        one = const.tile([P, 1], F32)
        nc.vector.memset(one[:], 1.0)
        one_half = const.tile([P, 1], F32)
        nc.gpsimd.memset(one_half[:], 0.5)
        ident = const.tile([P, P], F32)
        make_identity(nc, ident[:])
        tiny = const.tile([P, 1], F32)
        nc.gpsimd.memset(tiny[:], TINY)
        neg_half = const.tile([P, ROW_TILES], F32)
        nc.gpsimd.memset(neg_half[:], -0.5)
        neg_one = const.tile([P, 1], F32)
        nc.gpsimd.memset(neg_one[:], -1.0)
        warm = const.tile([P, 1], F32)
        nc.scalar.activation(out=warm[:], in_=one_half[:], func=ACT.Sqrt)

        def g_op(o, a, b, op):
            nc.gpsimd.tensor_tensor(out=o, in0=a, in1=b, op=op)

        def g_mul(o, a, b):
            g_op(o, a, b, ALU.mult)

        def g_pow(o, a, exponent):
            g_op(o, a, exponent, ALU.pow)

        def g_affine(o, a, mul, add):
            nc.gpsimd.tensor_scalar(out=o, in0=a, scalar1=mul, scalar2=add, op0=ALU.mult, op1=ALU.add)

        def g_one(o, a, scalar, op):
            nc.gpsimd.tensor_scalar(out=o, in0=a, scalar1=scalar, scalar2=None, op0=op)

        b2_all = const.tile([P, FEATS], F32)
        bn_parts = small.tile([P, HALVES], F32)

        def spread_b2():
            for h in range(HALVES):
                b2_bank = psum.tile([P, BANK], F32, tag="bank")
                cols = slice(h * BANK, (h + 1) * BANK)
                nc.tensor.matmul(out=b2_bank[:], lhsT=ones[:], rhs=b2_row[:, cols], start=True, stop=True)
                sq_b = unread.tile([P, BANK], BF16, name="sq_s")
                nc.scalar.activation(out=sq_b[:], in_=b2_bank[:], func=ACT.Square, accum_out=bn_parts[:, h : h + 1])
                nc.vector.tensor_copy(out=b2_all[:, cols], in_=b2_bank[:])

        bn = small.tile([P, 1], F32)
        inv_bn = small.tile([P, 1], F32)
        decay = small.tile([P, 1], F32)
        hb_norm = small.tile([P, 1], F32)
        hb_scale = small.tile([P, 1], F32)
        two_hb_scale = small.tile([P, 1], F32)
        y2 = small.tile([P, 1], F32)

        def bias_scalars():
            g_op(bn[:], bn_parts[:, 0:1], bn_parts[:, 1:2], ALU.add)
            g_one(bn[:], bn[:], MIN_NORM_SQ, ALU.max)
            g_pow(inv_bn[:], bn[:], neg_half[:, 0:1])
            g_mul(bn[:], bn[:], inv_bn[:])
            g_one(bn[:], bn[:], 2.0 / math.log(2.0), ALU.mult)
            g_pow(decay[:], one_half[:], bn[:])
            g_affine(hb_norm[:], decay[:], 1.0, 1.0)
            g_pow(hb_norm[:], hb_norm[:], neg_one[:, 0:1])
            g_affine(decay[:], decay[:], -1.0, 1.0)
            g_mul(hb_norm[:], hb_norm[:], decay[:])
            g_one(hb_norm[:], hb_norm[:], MAX_NORM, ALU.min)
            g_mul(hb_scale[:], hb_norm[:], inv_bn[:])
            g_one(two_hb_scale[:], hb_scale[:], 2.0, ALU.mult)
            g_mul(y2[:], hb_norm[:], hb_norm[:])

        def regroup(dst, src):
            nc.vector.tensor_copy(
                out=dst.rearrange("p (c i) t -> p c t i", i=4),
                in_=src.rearrange("p t (c i) -> p c t i", i=4),
            )

        def quantise(grouped, codes, scales):
            nc.vector.quantize_mx(out=codes.bitcast(FP8X4), scales=scales, in_=grouped)

        def flip(words, copy_out):
            flipped = psum.tile([P, 4, P], F32, tag="bank")
            for c in range(4):
                nc.tensor.transpose(out=flipped[:, c, :], in_=words[:, c * P : (c + 1) * P], identity=ident[:])
            grouped = rows_pool.tile([P, 2 * P * PACK], BF16, align_bytes=64)
            copy_out(
                out=grouped[:].bitcast(F32).rearrange("p (a r u) -> p a r u", a=2, u=2),
                in_=flipped[:].rearrange("p (a u) r -> p a r u", u=2),
            )
            return grouped

        w_codes = keep.tile([P, K_PASSES, FEATS], U32, align_bytes=64)
        w_scales = keep.tile([P, K_PASSES, FEATS], U8, align_bytes=64)
        w_grouped = {}

        def group_w(g, h):
            w_grouped[g, h] = stage.tile([P, BANK, PACK], BF16, align_bytes=64, name="w_grouped")
            regroup(w_grouped[g, h][:], w_raw[:, g, :, h * BANK : (h + 1) * BANK])

        def quantise_w(g, h):
            cols = slice(h * BANK, (h + 1) * BANK)
            quantise(w_grouped[g, h][:].rearrange("p c t -> p (c t)"), w_codes[:, g, cols], w_scales[:, g, cols])

        x_codes = keep.tile([P, ROW_TILES, K_PASSES * P], U32, align_bytes=64)
        x_scales = keep.tile([P, ROW_TILES, K_PASSES * P], U8, align_bytes=64)

        def project(col, first, width):
            acc = psum.tile([P, BANK], F32, tag="bank")
            cols = slice(first, first + width)
            for g in range(K_PASSES):
                nc.tensor.matmul_mx(
                    out=acc[:, 0:width],
                    lhsT=x_codes[:, col, g * P : (g + 1) * P].bitcast(FP8X4),
                    lhsT_scale=x_scales[:, col, g * P : (g + 1) * P],
                    rhs=w_codes[:, g, cols].bitcast(FP8X4),
                    rhs_scale=w_scales[:, g, cols],
                    start=(g == 0),
                    stop=(g == K_PASSES - 1),
                )
            return acc

        def locate(col):
            grp = GROUP_OF[col]
            return grp, col - GROUP_FIRST[grp]

        scalars = [{} for grp in range(GROUPS)]

        def single(grp, label):
            scalars[grp][label] = small.tile([P, GROUP_TILES[grp]], F32, name="%s%d" % (label, grp))
            return scalars[grp][label]

        def double(grp, label):
            scalars[grp][label] = small.tile([P, 2, GROUP_TILES[grp]], F32, name="%s%d" % (label, grp))
            return scalars[grp][label]

        def both(ap):
            return ap.unsqueeze(1).to_broadcast([P, 2, ap.shape[1]])

        xn = small.tile([P, ROW_TILES], F32)
        inv_xn = small.tile([P, ROW_TILES], F32)
        zb = small.tile([P, ROW_TILES], F32)
        one_plus = small.tile([P, ROW_TILES], F32)

        x_grouped = {}

        def square_x(col):
            sq_x = unread.tile([P, FEATS], BF16)
            nc.scalar.activation(out=sq_x[:], in_=x_nat[:, col, :], func=ACT.Square, accum_out=xn[:, col : col + 1])

        def flip_x(col, copy_out):
            x_grouped[col] = flip(x_nat[:, col, :].bitcast(F32), copy_out)

        def gram_x(col):
            gram = psum.tile([P, BANK], F32, tag="bank")
            chunks = x_grouped[col][:].rearrange("p (a r t) -> p a t r", a=K_PASSES, t=PACK)
            for c in range(K_PASSES * PACK):
                a, t = divmod(c, PACK)
                nc.tensor.matmul(
                    out=gram[:, 0:P], lhsT=chunks[:, a, t, :], rhs=chunks[:, a, t, :],
                    start=(c == 0), stop=(c == K_PASSES * PACK - 1),
                )
            return gram

        def diagonal(col, gram):
            picked = unread.tile([P, P], F32)
            nc.vector.scalar_tensor_tensor(
                out=picked[:], in0=gram[:, 0:P], scalar=1.0, in1=ident[:],
                op0=ALU.mult, op1=ALU.mult, accum_out=xn[:, col : col + 1],
            )

        def quantise_x(col):
            quantise(x_grouped[col][:], x_codes[:, col, :], x_scales[:, col, :])

        def v_op(o, a, b, op):
            nc.vector.tensor_tensor(out=o, in0=a, in1=b, op=op)

        def x_scalars():
            nc.scalar.activation(out=xn[:], in_=xn[:], func=ACT.Sqrt, scale=1.0, bias=tiny[:, 0:1])
            g_one(zb[:], xn[:], ARTANH_CLIP, ALU.min)
            g_affine(one_plus[:], zb[:], 1.0, 1.0)
            g_affine(zb[:], zb[:], -1.0, 1.0)

        def x_ratio():
            nc.vector.reciprocal(out=inv_xn[:], in_=xn[:])
            nc.vector.reciprocal(out=one_plus[:], in_=one_plus[:])
            g_mul(zb[:], zb[:], one_plus[:])

        for grp in range(GROUPS):
            scalars[grp]["parts"] = small.tile([P, HALVES, 2, GROUP_TILES[grp]], F32, name="parts%d" % grp)

        def dot_hb(col, h, acc):
            grp, i = locate(col)
            prod_v = unread.tile([P, BANK], F32)
            nc.vector.scalar_tensor_tensor(
                out=prod_v[:], in0=acc[:], scalar=2.0, in1=b2_all[:, h * BANK : (h + 1) * BANK],
                op0=ALU.mult, op1=ALU.mult, accum_out=scalars[grp]["parts"][:, h, 1, i : i + 1],
            )

        def square_mx(col, h, acc):
            grp, i = locate(col)
            sq_s = unread.tile([P, BANK], BF16)
            nc.scalar.activation(out=sq_s[:], in_=acc[:], func=ACT.Square, accum_out=scalars[grp]["parts"][:, h, 0, i : i + 1])

        def v_mul(o, a, b):
            nc.vector.tensor_tensor(out=o, in0=a, in1=b, op=ALU.mult)

        def v_two(o, a, scalar, b):
            nc.vector.scalar_tensor_tensor(out=o, in0=a, scalar=scalar, in1=b, op0=ALU.mult, op1=ALU.mult)

        def sum_mx(grp):
            parts = scalars[grp]["parts"]
            mn_e2 = double(grp, "mn_e2")
            g_op(mn_e2[:], parts[:, 0], parts[:, 1], ALU.add)

        def root_mx(grp):
            mn_e2 = scalars[grp]["mn_e2"]
            if grp == 0:
                nc.scalar.activation(out=mn_e2[:, 0, :], in_=mn_e2[:, 0, :], func=ACT.Sqrt, scale=1.0, bias=tiny[:, 0:1])

        def start_scalars(grp):
            got = scalars[grp]
            n = GROUP_TILES[grp]
            mine = slice(GROUP_FIRST[grp], GROUP_FIRST[grp] + n)
            mn, e2 = got["mn_e2"][:, 0, :], got["mn_e2"][:, 1, :]
            inv_mn = single(grp, "inv_mn")
            if grp == 0:
                nc.vector.reciprocal(out=inv_mn[:], in_=mn)
            else:
                g_one(mn, mn, TINY, ALU.max)
                g_pow(inv_mn[:], mn, neg_half[:, 0:n])
                g_mul(mn, mn, inv_mn[:])
            z = single(grp, "z")
            g_mul(z[:], mn, inv_xn[:, mine])
            g_pow(z[:], zb[:, mine], z[:])
            p_q = double(grp, "p_q")
            p, q = p_q[:, 0, :], p_q[:, 1, :]
            g_affine(p, z[:], -1.0, 1.0)
            g_affine(q, z[:], 1.0, 1.0)
            squares = double(grp, "squares")
            g_mul(squares[:], p_q[:], p_q[:])
            c1 = single(grp, "c1")
            g_mul(c1[:], p, q)
            g_mul(e2, e2, inv_mn[:])
            g_one(e2, e2, hb_scale[:, 0:1], ALU.mult)
            g_mul(c1[:], c1[:], e2)
            times_y2 = double(grp, "times_y2")
            g_one(times_y2[:], squares[:], y2[:, 0:1], ALU.mult)
            plus_c1 = double(grp, "plus_c1")
            g_op(plus_c1[:], squares[:], both(c1[:]), ALU.add)
            den = single(grp, "den")
            g_op(den[:], plus_c1[:, 1, :], times_y2[:, 0, :], ALU.add)
            nums = double(grp, "nums")
            g_op(nums[:], plus_c1[:], both(times_y2[:, 1, :]), ALU.add)
            g_mul(den[:], den[:], nums[:, 0, :])
            g_mul(den[:], den[:], squares[:, 1, :])

        def root_scalars(grp):
            got = scalars[grp]
            n = GROUP_TILES[grp]
            den = got["den"]
            inv_q_den_sn = single(grp, "inv_q_den_sn")
            g_one(den[:], den[:], TINY, ALU.max)
            g_pow(inv_q_den_sn[:], den[:], neg_half[:, 0:n])

        def late_ops(grp):
            got = scalars[grp]
            inv_den_sn = single(grp, "inv_den_sn")
            sn = single(grp, "sn")
            logs = double(grp, "logs")
            alpha_beta = double(grp, "alpha_beta")
            alpha, beta = alpha_beta[:, 0, :], alpha_beta[:, 1, :]
            log_ratio = single(grp, "log_ratio")
            w = got["inv_q_den_sn"]

            def take_logs():
                nc.scalar.activation(out=logs[:, 0, :], in_=sn[:], func=ACT.Ln, scale=1.0, bias=one[:, 0:1])
                nc.scalar.activation(out=logs[:, 1, :], in_=sn[:], func=ACT.Ln, scale=-1.0, bias=one[:, 0:1])

            def least():
                nc.vector.tensor_scalar(out=sn[:], in0=sn[:], scalar1=MAX_NORM, scalar2=None, op0=ALU.min)
                take_logs()

            return [
                lambda: v_mul(inv_den_sn[:], w[:], got["p_q"][:, 1, :]),
                lambda: v_two(alpha, got["nums"][:, 1, :], 0.5, got["p_q"][:, 0, :]),
                lambda: v_mul(sn[:], got["nums"][:, 0, :], inv_den_sn[:]),
                lambda: v_two(beta, got["z"][:], two_hb_scale[:, 0:1], inv_den_sn[:]),
                least,
                lambda: v_mul(alpha, alpha, got["inv_mn"][:]),
                lambda: v_mul(alpha, alpha, w[:]),
                lambda: v_op(log_ratio[:], logs[:, 0, :], logs[:, 1, :], ALU.subtract),
                lambda: v_mul(alpha_beta[:], alpha_beta[:], both(log_ratio[:])),
            ]

        def residual(grp):
            sum_mx(grp)
            start_scalars(grp)
            root_scalars(grp)

        a_codes = keep.tile([P, GRAPHS, NODES], U32, align_bytes=64)
        a_scales = keep.tile([P, GRAPHS, NODES], U8, align_bytes=64)
        a_grouped = {}

        def flip_adj(b, pair, copy_out):
            words = a_nat[:, b, 2 * pair : 2 * pair + 2, :].rearrange("p m j -> p (m j)").bitcast(F32)
            a_grouped[b, pair] = flip(words, copy_out)

        def quantise_adj(b, pair):
            cols = slice(pair * 2 * P, (pair + 1) * 2 * P)
            quantise(a_grouped[b, pair][:], a_codes[:, b, cols], a_scales[:, b, cols])

        UNIT_LIST = [(b, h * BANK, BANK) for b in range(GRAPHS) for h in range(HALVES)]
        UNITS = len(UNIT_LIST)
        tangent = [{} for j in range(UNITS)]

        def spread_bias(j, t):
            b, first, width = UNIT_LIST[j]
            grp, i = locate(b * TILES_PER_GRAPH + t)
            beta_hb = bias_pool.tile([P, BANK], F32)
            nc.scalar.activation(
                out=beta_hb[:, 0:width], in_=b2_all[:, first : first + width], func=ACT.Copy,
                scale=scalars[grp]["alpha_beta"][:, 1, i : i + 1],
            )
            tangent[j]["bias", t] = beta_hb

        def tangent_tile(j, t):
            b, first, width = UNIT_LIST[j]
            if t == 0:
                tangent[j]["planes"] = planes_pool.tile([P, PACK, BANK], BF16, name="planes")
            grp, i = locate(b * TILES_PER_GRAPH + t)
            acc = project(b * TILES_PER_GRAPH + t, first, width)
            nc.vector.scalar_tensor_tensor(
                out=tangent[j]["planes"][:, t, 0:width], in0=acc[:, 0:width],
                scalar=scalars[grp]["alpha_beta"][:, 0, i : i + 1],
                in1=tangent[j]["bias", t][:, 0:width], op0=ALU.mult, op1=ALU.add,
            )

        def group_tangent(j):
            width = UNIT_LIST[j][2]
            tangent[j]["grouped"] = tan_pool.tile([P, BANK, PACK], BF16, align_bytes=64, name="t_grouped")
            dst, src = tangent[j]["grouped"][:, 0:width, :], tangent[j]["planes"][:, :, 0:width]
            copy = nc.scalar.copy if j in SRG else nc.vector.tensor_copy
            copy(
                out=dst.rearrange("p (c i) t -> p c t i", i=4),
                in_=src.rearrange("p t (c i) -> p c t i", i=4),
            )

        def quantise_tangent(j):
            width = UNIT_LIST[j][2]
            tangent[j]["codes"] = tan_pool.tile([P, BANK], U32, align_bytes=64, name="t_codes")
            tangent[j]["scales"] = tan_pool.tile([P, BANK], U8, align_bytes=64, name="t_scales")
            quantise(
                tangent[j]["grouped"][:, 0:width, :].rearrange("p c t -> p (c t)"),
                tangent[j]["codes"][:, 0:width], tangent[j]["scales"][:, 0:width],
            )

        def aggregate_tile(j, m):
            b, first, width = UNIT_LIST[j]
            if m % 2 == 0:
                tangent[j]["result"] = out_pool.tile([P, 2, BANK], F32, name="result")
            result = tangent[j]["result"]
            agg = psum.tile([P, BANK], F32, tag="bank")
            nc.tensor.matmul_mx(
                out=agg[:, 0:width],
                lhsT=a_codes[:, b, m * P : (m + 1) * P].bitcast(FP8X4),
                lhsT_scale=a_scales[:, b, m * P : (m + 1) * P],
                rhs=tangent[j]["codes"][:, 0:width].bitcast(FP8X4),
                rhs_scale=tangent[j]["scales"][:, 0:width],
                start=True,
                stop=True,
            )
            if (j == UNITS - 1 and m % 2 == 1):
                nc.vector.tensor_scalar(out=result[:, m % 2, 0:width], in0=agg[:, 0:width], scalar1=0.0, scalar2=None, op0=ALU.max)
            else:
                nc.scalar.activation(out=result[:, m % 2, 0:width], in_=agg[:, 0:width], func=ACT.Relu)
            view = out[b].rearrange("(p m) f -> p m f", m=TILES_PER_GRAPH)[:, :, first : first + width]
            if j == UNITS - 1:
                nc.sync.dma_start(out=view[:, m, :], in_=result[:, m % 2, 0:width])
            elif m % 2 == 1:
                nc.sync.dma_start(out=view[:, m - 1 : m + 1, :], in_=result[:, :, 0:width])

        square_x(0)
        flip_x(0, nc.scalar.copy)
        square_x(1)
        flip_x(1, nc.scalar.copy)
        group_w(0, 0)
        group_w(0, 1)
        quantise_w(0, 0)
        quantise_w(0, 1)
        quantise_x(0)

        grams = {}

        def prepare(col):
            if col < ROW_TILES:
                if col not in GRAM:
                    square_x(col)
                flip_x(col, nc.scalar.copy if col in FS else nc.vector.tensor_copy)
            if 1 <= col - 1 < ROW_TILES:
                quantise_x(col - 1)
            if 1 <= col - 2 < ROW_TILES:
                if col - 2 in GRAM:
                    grams[col - 2] = gram_x(col - 2)
            if col - 3 in grams:
                diagonal(col - 3, grams[col - 3])

        LEAD = 19
        VRELU = ()
        FS = (2,3,5,7,9,11,13,15)
        GRAM = (5,7,9,11,13)
        for col in range(2, LEAD):
            prepare(col)
            if col == 6:
                spread_b2()
                bias_scalars()
            if col == 3:
                group_w(1, 0)
            if col == 4:
                group_w(1, 1)
                quantise_w(1, 0)
            if col == 5:
                quantise_w(1, 1)

        for col in range(ROW_TILES):
            acc = [project(col, h * BANK, BANK) for h in range(HALVES)]
            for h in range(HALVES):
                dot_hb(col, h, acc[h])
                square_mx(col, h, acc[h])
            if LEAD + col < ROW_TILES + 3:
                prepare(LEAD + col)
            if col == 0:
                x_scalars()
            if col == 2:
                x_ratio()
            if col == 7:
                sum_mx(0)
            if col == 8:
                root_mx(0)
                start_scalars(0)
                root_scalars(0)
            if col == 10:
                nc.scalar.activation(out=warm[:], in_=one_half[:], func=ACT.Ln)
            if col == 14:
                ops = late_ops(0)
            if 14 <= col:
                for k in ((0, 2, 1, 4, 3), (5, 7, 6, 8))[col - 14]:
                    ops[k]()
        residual(1)
        SRG = (2,)
        SC, VC = nc.scalar.copy, nc.vector.tensor_copy
        FLIPS = {(0, 1): (2, 0, VC), (0, 3): (2, 1, VC), (1, 1): (1, 0, SC), (1, 3): (1, 1, SC), (2, 1): (3, 0, SC), (2, 3): (3, 1, SC)}
        for t in range(TILES_PER_GRAPH):
            spread_bias(0, t)
        for pair in range(2):
            flip_adj(0, pair, nc.scalar.copy)
        for t in range(TILES_PER_GRAPH):
            spread_bias(1, t)
        order = (0, 2, 1, 4, 3, 5, 7, 6, 8)
        for j in range(UNITS + 1):
            b, h = divmod(j, HALVES)
            for t in range(TILES_PER_GRAPH):
                if j < UNITS:
                    tangent_tile(j, t)
                if (j, t) in FLIPS:
                    flip_adj(FLIPS[j, t][0], FLIPS[j, t][1], FLIPS[j, t][2])
                if j > 0 and t == 0:
                    group_tangent(j - 1)
                if j == 0 and t == 3:
                    quantise_adj(0, 0)
                    quantise_adj(0, 1)
                if j > 0 and t == 2:
                    quantise_tangent(j - 1)
                if j > 2 and j < UNITS and h == 1 and t in (1, 3):
                    quantise_adj(b + 0, t // 2)
                if j >= 2:
                    aggregate_tile(j - 2, t)
                if j == 0:
                    spread_bias(2, t)
                if j == 1:
                    spread_bias(3, t)
                if j == 3:
                    if t == 0:
                        late = late_ops(1)
                    for k in (order[0:2], order[2:4], order[4:6], order[6:9])[t]:
                        late[k]()
                if j == 3 and t == 3:
                    for k in range(TILES_PER_GRAPH):
                        spread_bias(4, k)
                if 4 <= j and j + 1 < UNITS:
                    spread_bias(j + 1, t)
        for t in range(TILES_PER_GRAPH):
            aggregate_tile(UNITS - 1, t)
